import numpy as np
import ml_dtypes


def mxq(x, axis, fmt="e4m3"):
    dtype, down = {"e4m3": (ml_dtypes.float8_e4m3fn, 7), "e5m2": (ml_dtypes.float8_e5m2, 14)}[fmt]
    v = np.moveaxis(np.asarray(x, np.float32).astype(ml_dtypes.bfloat16).astype(np.float64), axis, -1)
    blocks = v.reshape(v.shape[:-1] + (-1, 32))
    amax = np.abs(blocks).max(-1, keepdims=True)
    byte = np.maximum(np.where(amax > 0, np.frexp(amax)[1] - 1 + 127, 0) - down, 1)
    scale = np.exp2(byte - 127.0)
    codes = (blocks / scale).astype(np.float32).astype(dtype).astype(np.float64)
    return np.moveaxis((codes * scale).reshape(v.shape), -1, axis)


WIDE = False


def mx_kscale(k):
    if not WIDE:
        return np.ones(k)
    levels = np.array([10, -10, 5, -5, 0])
    if k % 512:
        return np.exp2(np.random.permutation(np.resize(levels, k // 32))).repeat(32)
    a = np.empty((k // 512, 16))
    for p in range(k // 512):
        a[p, :8] = np.random.permutation(np.resize(levels, 8))
        for g in range(8):
            far = levels[np.abs(levels - a[p, g]) >= 10]
            a[p, g + 8] = far[np.random.randint(len(far))]
    return np.exp2(a.ravel()).repeat(32)


BF16 = ml_dtypes.bfloat16


def bf(x):
    return np.asarray(x, np.float32).astype(BF16)


def f64(x):
    return np.asarray(x).astype(np.float64)


B, P, D = 2048, 2, 512
IN = P * D


def sigmoid(v):
    return 1.0 / (1.0 + np.exp(-v))


def pre_activation(x, weights, bias, gain, norm_bias):
    xn = f64(x) * f64(gain) + f64(norm_bias)
    yp = xn.reshape(B, P, D).transpose(1, 0, 2) @ f64(weights)
    return yp.transpose(1, 0, 2).reshape(B, IN) + f64(bias)


def setup_inputs():
    s = mx_kscale(B)[:, None]
    u = mx_kscale(D)
    uf = np.tile(u, P)
    x0 = bf(np.random.standard_normal((B, IN)))
    w0 = bf(np.random.standard_normal((P, D, D)) / np.sqrt(D))
    bias = bf(np.random.standard_normal(IN) * 0.3)
    gain = bf(1.3 + 0.1 * np.random.standard_normal(1))
    nb0 = bf(0.3 + 0.05 * np.random.standard_normal(1))
    gamma = bf(0.5 + 0.3 * np.random.standard_normal(IN))
    beta = bf(np.random.standard_normal(IN))
    g = bf(np.random.standard_normal((B, IN)) * np.exp2(np.random.randint(-6, 1, (B, 1))) * 2.0 / s * uf)
    y = pre_activation(x0, w0, bias, gain, nb0)
    return {"x": bf(f64(x0) * s),
            "weights": bf(f64(w0) * u[None, :, None] / u[None, None, :]),
            "bias": bias, "gain": gain, "norm_bias": bf(f64(nb0) * s.min()),
            "gamma": gamma, "beta": beta,
            "y": np.asarray(y, np.float32), "grad_out": g}


def reference(x, weights, bias, gain, norm_bias, gamma, beta, y, grad_out):
    g, yf, ga, be = f64(grad_out), f64(y), f64(gamma), f64(beta)
    sg = sigmoid(be * yf)
    dy = g * (ga + (1.0 - ga) * sg * (1.0 + be * yf * (1.0 - sg)))
    dyp = dy.reshape(B, P, D).transpose(1, 0, 2)
    x_norm = f64(x) * f64(gain) + f64(norm_bias)
    xp = x_norm.reshape(B, P, D).transpose(1, 0, 2)
    dxp = mxq(dyp, 2, "e5m2") @ mxq(f64(weights), 2, "e4m3").transpose(0, 2, 1)
    dw = mxq(xp, 1, "e4m3").transpose(0, 2, 1) @ mxq(dyp, 1, "e5m2")
    dx = dxp.transpose(1, 0, 2).reshape(B, IN) * f64(gain) + g
    return dx, dw

@@ -1,0 +1,459 @@
+from contextlib import ExitStack
+
+import concourse.mybir as mybir
+from concourse.masks import make_identity
+
+FLOPS = 2 * 2 * 2 * 2048 * 512 * 512
+
+F32 = mybir.dt.float32
+BF16 = mybir.dt.bfloat16
+U32 = mybir.dt.uint32
+U8 = mybir.dt.uint8
+E4 = mybir.dt.float8_e4m3fn_x4
+E5 = mybir.dt.float8_e5m2_x4
+ACT = mybir.ActivationFunctionType
+ALU = mybir.AluOpType
+
+P = 128
+PACK = 4
+D = 512
+PARTS = 2
+NG = 4
+NCH = PARTS * NG
+NB = NCH * PACK
+
+MANUAL = False
+BP_S = []
+BP_G = []
+XN_ENG = "s"
+IL_V_COLS = 192
+IL_REST = "s"
+EV_ENG = "s"
+Y_BUFS = 4
+G_BUFS = 5
+X_BUFS = 3
+
+
+def tile_better_transformer_t_v_kernel(
+    tc, x, weights, bias, gain, norm_bias, gamma, beta, y, grad_out, out_0, out_1
+):
+    nc = tc.nc
+
+    y_v = y.rearrange("(g p j) w -> p g j w", p=P, j=PACK)
+    g_v = grad_out.rearrange("(g p j) w -> p g j w", p=P, j=PACK)
+    x_v = x.rearrange("(g p j) w -> p g j w", p=P, j=PACK)
+    o0_v = out_0.rearrange("(g p j) w -> p g j w", p=P, j=PACK)
+    w_v = weights.rearrange("a (t p) o -> p a t o", p=P)
+
+    with ExitStack() as ctx:
+        if MANUAL:
+            ctx.enter_context(tc.manual_schedule())
+        const = ctx.enter_context(tc.tile_pool(name="const", bufs=1))
+        keep = ctx.enter_context(tc.tile_pool(name="keep", bufs=1))
+        raw = ctx.enter_context(tc.tile_pool(name="raw", bufs=2))
+        work = ctx.enter_context(tc.tile_pool(name="work", bufs=2))
+        psum = ctx.enter_context(tc.psum_pool(name="psum", bufs=2))
+
+        y_t = {}
+        g_t = {}
+        x_t = {}
+
+        def cols(part):
+            return slice(part * D, (part + 1) * D)
+
+        def load_y0():
+            for b in range(PACK):
+                t = raw.tile([P, PACK, P], F32, name="y_first", tag="y0", bufs=PACK)
+                nc.sync.dma_start(out=t[:], in_=y_v[:, 0, :, b * P : (b + 1) * P])
+                y_t[(0, b)] = t
+
+        def load_y(c):
+            part, g = divmod(c, NG)
+            t = raw.tile([P, PACK, D], F32, name="y_raw", tag="y", bufs=Y_BUFS)
+            nc.sync.dma_start(out=t[:], in_=y_v[:, g, :, cols(part)])
+            y_t[c] = t
+
+        def y_block(c, b, j):
+            if c == 0:
+                return y_t[(0, b)][:, j, :]
+            return y_t[c][:, j, b * P : (b + 1) * P]
+
+        def load_g(c):
+            part, g = divmod(c, NG)
+            t = raw.tile([P, PACK, D], BF16, name="g_raw", tag="g", bufs=G_BUFS)
+            nc.sync.dma_start(out=t[:], in_=g_v[:, g, :, cols(part)])
+            g_t[c] = t
+
+        def load_x(c):
+            part, g = divmod(c, NG)
+            t = raw.tile([P, PACK, D], BF16, name="x_raw", tag="x", bufs=X_BUFS)
+            nc.sync.dma_start(out=t[:], in_=x_v[:, g, :, cols(part)])
+            x_t[c] = t
+
+        w_raw = []
+
+        def load_w(part):
+            t = const.tile([P, PACK, D], BF16, name="w_raw%d" % part)
+            nc.sync.dma_start(out=t[:], in_=w_v[:, part, :, :])
+            w_raw.append(t)
+
+        junk = const.tile([P, 1], F32, name="junk")
+        nc.vector.memset(junk[:], 0.0)
+        vecs = const.tile([P, P], BF16, name="vecs")
+        nc.vector.memset(vecs[:], 0.0)
+        nc.scalar.dma_start(out=vecs[0:8, :], in_=beta.rearrange("(c f) -> c f", f=P))
+        nc.scalar.dma_start(out=vecs[8:16, :], in_=gamma.rearrange("(c f) -> c f", f=P))
+        gain_b = const.tile([P, 1], BF16, name="gain_b")
+        nc.scalar.dma_start(out=gain_b[:], in_=gain.partition_broadcast(P))
+        nb_b = const.tile([P, 1], BF16, name="nb_b")
+        nc.scalar.dma_start(out=nb_b[:], in_=norm_bias.partition_broadcast(P))
+        junk2 = const.tile([P, 1], F32, name="junk2")
+        nc.scalar.activation(out=junk2[:], in_=junk[:], func=ACT.Silu)
+
+        load_y0()
+        load_g(0)
+        load_y(1)
+        load_w(0)
+        load_g(1)
+        load_y(2)
+        load_w(1)
+        load_x(0)
+        load_g(2)
+        load_x(1)
+        load_y(3)
+        load_g(3)
+        load_x(2)
+        load_y(4)
+        load_g(4)
+
+        ident_f = const.tile([P, P], F32, name="ident_f")
+        make_identity(nc, ident_f[:])
+        ident_b = const.tile([P, P], BF16, name="ident_b")
+        make_identity(nc, ident_b[:])
+
+        vecs_T = psum.tile([P, P], BF16, name="vecs_T", tag="wT")
+        nc.tensor.transpose(vecs_T[:], vecs[:], ident_b[:])
+        be = const.tile([P, 8], F32, name="be")
+        nc.vector.tensor_copy(out=be[:], in_=vecs_T[:, 0:8])
+        hbe = const.tile([P, 8], F32, name="hbe")
+        nc.vector.tensor_scalar(out=hbe[:], in0=vecs_T[:, 0:8], scalar1=0.5, scalar2=None, op0=ALU.mult)
+        cneg = const.tile([P, 8], F32, name="cneg")
+        nc.vector.tensor_scalar(
+            out=cneg[:], in0=vecs_T[:, 8:16], scalar1=-1.0, scalar2=0.5, op0=ALU.add, op1=ALU.mult
+        )
+        mcneg = const.tile([P, 8], F32, name="mcneg")
+        nc.vector.tensor_scalar(
+            out=mcneg[:], in0=vecs_T[:, 8:16], scalar1=-1.0, scalar2=-0.5, op0=ALU.add, op1=ALU.mult
+        )
+        gain_c = const.tile([P, 1], F32, name="gain_c")
+        nc.vector.tensor_copy(out=gain_c[:], in_=gain_b[:])
+        nb_c = const.tile([P, 1], F32, name="nb_c")
+        nc.vector.tensor_copy(out=nb_c[:], in_=nb_b[:])
+
+        def words_out(dst, bank, eng):
+            dw = dst.rearrange("p r t -> p (r t)").bitcast(F32).rearrange("p (r u) -> p r u", u=2)
+            src = bank.rearrange("p u r -> p r u")
+            if eng == "s":
+                nc.scalar.copy(out=dw, in_=src)
+            else:
+                nc.vector.tensor_copy(out=dw, in_=src)
+
+        def interleave(dst, src, eng):
+            if eng == "v":
+                nc.vector.tensor_copy(out=dst, in_=src)
+            elif eng == "s":
+                nc.scalar.copy(out=dst, in_=src)
+            else:
+                nc.gpsimd.tensor_scalar(out=dst, in0=src, scalar1=1.0, scalar2=0.0, op0=ALU.mult, op1=ALU.add)
+
+        w_bank = {}
+        w_g = {}
+        w_q = {}
+
+        def w_pe(part):
+            w_g[part] = work.tile([P, D, PACK], BF16, name="wg", tag="wg", bufs=2, align_bytes=64)
+            for h in range(2):
+                bank = psum.tile([P, 2, 2 * P], F32, name="w_T", tag="wT")
+                for u in range(2):
+                    for t2 in range(2):
+                        ww = w_raw[part][:, 2 * h + t2, :].bitcast(F32)
+                        nc.tensor.transpose(bank[:, u, t2 * P : (t2 + 1) * P], ww[:, u : D // 2 : 2], ident_f[:])
+                w_bank[(part, h)] = bank
+
+        def w_ev(part, h, eng):
+            words_out(w_g[part][:, h * 2 * P : (h + 1) * 2 * P, :], w_bank.pop((part, h))[:], eng)
+
+        def w_quant(part):
+            wc = keep.tile([P, D], U32, name="w_codes%d" % part, align_bytes=64)
+            ws = keep.tile([P, D], U8, name="w_scales%d" % part, align_bytes=64)
+            nc.vector.quantize_mx(
+                out=wc[:].bitcast(E4), scales=ws[:], in_=w_g[part][:].rearrange("p r t -> p (r t)")
+            )
+            w_q[part] = (wc, ws)
+
+        yT = {}
+        th_t = {}
+        s1_t = {}
+        mT = {}
+        dn_t = {}
+        dq_t = {}
+        tg_t = {}
+        dT_bank = {}
+        dyk = {}
+        xq_t = {}
+        xk = {}
+        dyT = {}
+        acc0 = {}
+
+        def pe_yt(k):
+            c, b = divmod(k, PACK)
+            bank = psum.tile([P, PACK, P], F32, name="y_T", tag="yT")
+            for j in range(PACK):
+                nc.tensor.transpose(bank[:, j, :], y_block(c, b, j), ident_f[:])
+            yT[k] = bank
+
+        def s_act(k):
+            flat = yT.pop(k)[:].rearrange("p j t -> p (j t)")
+            th = work.tile([P, D], F32, name="th", tag="th", bufs=5)
+            col = (k // PACK // NG) * PACK + k % PACK
+            nc.scalar.activation(out=th[:], in_=flat, func=ACT.Tanh, scale=hbe[:, col : col + 1])
+            s1 = work.tile([P, D], F32, name="s1", tag="s1", bufs=4)
+            nc.scalar.activation(out=s1[:], in_=flat, func=ACT.Silu, scale=be[:, col : col + 1])
+            if k % PACK in BP_S:
+                nc.scalar.activation(
+                    out=s1[:], in_=s1[:], func=ACT.Identity, scale=cneg[:, col : col + 1], bias=mcneg[:, col : col + 1]
+                )
+            elif k % PACK in BP_G:
+                nc.gpsimd.tensor_scalar(
+                    out=s1[:], in0=s1[:], scalar1=-1.0, scalar2=cneg[:, col : col + 1], op0=ALU.add, op1=ALU.mult
+                )
+            th_t[k] = th
+            s1_t[k] = s1
+
+        def v_bp(k):
+            col = (k // PACK // NG) * PACK + k % PACK
+            s1 = s1_t[k]
+            if k % PACK not in BP_S and k % PACK not in BP_G:
+                nc.vector.tensor_scalar(
+                    out=s1[:], in0=s1[:], scalar1=-1.0, scalar2=cneg[:, col : col + 1], op0=ALU.add, op1=ALU.mult
+                )
+
+        def v_m(k):
+            th = th_t[k]
+            s1 = s1_t.pop(k)
+            nc.vector.scalar_tensor_tensor(out=th[:], in0=th[:], scalar=-1.0, in1=s1[:], op0=ALU.add, op1=ALU.mult)
+
+        def pe_mt(k):
+            bank = psum.tile([P, PACK, P], F32, name="m_T", tag="mT")
+            th = th_t.pop(k)
+            for j in range(PACK):
+                nc.tensor.transpose(bank[:, j, :], th[:, j * P : (j + 1) * P], ident_f[:])
+            mT[k] = bank
+
+        def v_dy(k):
+            c, b = divmod(k, PACK)
+            if b == 0:
+                dn_t[c] = work.tile([P, PACK, D], BF16, name="dn", tag="dn", bufs=2, align_bytes=64)
+            nc.vector.scalar_tensor_tensor(
+                out=dn_t[c][:, :, b * P : (b + 1) * P],
+                in0=mT.pop(k)[:],
+                scalar=1.0,
+                in1=g_t[c][:, :, b * P : (b + 1) * P],
+                op0=ALU.add,
+                op1=ALU.mult,
+            )
+
+        def pe_e(c):
+            words = dn_t[c][:].rearrange("p j c -> p (j c)").bitcast(F32)
+            tg_t[c] = work.tile([P, D, PACK], BF16, name="dyTg", tag="dyTg", bufs=2, align_bytes=64)
+            for jp in range(2):
+                bank = psum.tile([P, 2, 2 * P], F32, name="d_T", tag="wT")
+                for u in range(2):
+                    for j2 in range(2):
+                        j = 2 * jp + j2
+                        nc.tensor.transpose(
+                            bank[:, u, j2 * P : (j2 + 1) * P],
+                            words[:, j * (D // 2) + u : (j + 1) * (D // 2) : 2],
+                            ident_f[:],
+                        )
+                dT_bank[(c, jp)] = bank
+
+        def ev(c, jp):
+            words_out(tg_t[c][:, jp * 2 * P : (jp + 1) * 2 * P, :], dT_bank.pop((c, jp))[:], EV_ENG)
+
+        def v_q_dyT(c):
+            tcod = work.tile([P, D], U32, name="dyT_codes", tag="dyTc", bufs=2, align_bytes=64)
+            tsc = work.tile([P, D], U8, name="dyT_scales", tag="dyTs", bufs=2, align_bytes=64)
+            nc.vector.quantize_mx(
+                out=tcod[:].bitcast(E5), scales=tsc[:], in_=tg_t.pop(c)[:].rearrange("p r t -> p (r t)")
+            )
+            dyT[c] = (tcod, tsc)
+
+        def il(c, lo, hi, eng):
+            if c not in dq_t:
+                dq_t[c] = work.tile([P, D, PACK], BF16, name="dq", tag="dq", bufs=2, align_bytes=64)
+            if hi > lo:
+                interleave(dq_t[c][:, lo:hi, :], dn_t[c][:, :, lo:hi].rearrange("p j c -> p c j"), eng)
+
+        def v_q_dq(c):
+            kc = keep.tile([P, D], U32, name="dyk_codes%d" % c, align_bytes=64)
+            ks = keep.tile([P, D], U8, name="dyk_scales%d" % c, align_bytes=64)
+            nc.vector.quantize_mx(
+                out=kc[:].bitcast(E5), scales=ks[:], in_=dq_t.pop(c)[:].rearrange("p c j -> p (c j)")
+            )
+            dyk[c] = (kc, ks)
+
+        def pe_mx0(c, j):
+            part = c // NG
+            tcod, tsc = dyT[c]
+            acc = psum.tile([P, D], F32, name="acc0", tag="acc")
+            nc.tensor.matmul_mx(
+                out=acc[:],
+                lhsT=tcod[:, j * P : (j + 1) * P].bitcast(E5),
+                lhsT_scale=tsc[:, j * P : (j + 1) * P],
+                rhs=w_q[part][0][:].bitcast(E4),
+                rhs_scale=w_q[part][1][:],
+                start=True,
+                stop=True,
+            )
+            acc0[(c, j)] = acc
+
+        def v_e0(c, j):
+            part, g = divmod(c, NG)
+            o0 = work.tile([P, D], F32, name="o0", tag="o0", bufs=6)
+            nc.vector.scalar_tensor_tensor(
+                out=o0[:], in0=acc0.pop((c, j))[:], scalar=gain_c[:, 0:1], in1=g_t[c][:, j, :], op0=ALU.mult, op1=ALU.add
+            )
+            nc.sync.dma_start(out=o0_v[:, g, j, cols(part)], in_=o0[:])
+
+        def xn(c, h):
+            if h == 0:
+                xq_t[c] = work.tile([P, D, PACK], BF16, name="xq", tag="xq", bufs=2, align_bytes=64)
+            lo = h * (D // 2)
+            hi = lo + D // 2
+            dst = xq_t[c][:, lo:hi, :]
+            src = x_t[c][:, :, lo:hi].rearrange("p j c -> p c j")
+            if XN_ENG == "s":
+                nc.scalar.activation(out=dst, in_=src, func=ACT.Identity, scale=gain_c[:, 0:1], bias=nb_c[:, 0:1])
+            elif XN_ENG == "v":
+                nc.vector.tensor_scalar(
+                    out=dst, in0=src, scalar1=gain_c[:, 0:1], scalar2=nb_c[:, 0:1], op0=ALU.mult, op1=ALU.add
+                )
+            else:
+                nc.gpsimd.tensor_scalar(
+                    out=dst, in0=src, scalar1=gain_c[:, 0:1], scalar2=nb_c[:, 0:1], op0=ALU.mult, op1=ALU.add
+                )
+
+        def v_q_x(c):
+            kc = keep.tile([P, D], U32, name="xk_codes%d" % c, align_bytes=64)
+            ks = keep.tile([P, D], U8, name="xk_scales%d" % c, align_bytes=64)
+            nc.vector.quantize_mx(
+                out=kc[:].bitcast(E4), scales=ks[:], in_=xq_t.pop(c)[:].rearrange("p c j -> p (c j)")
+            )
+            xk[c] = (kc, ks)
+
+        acc1 = {}
+
+        def pe_o(part, it, g_lo, g_hi, tag):
+            if g_lo == 0:
+                acc1[(part, it)] = psum.tile([P, D], F32, name="acc1", tag=tag)
+            acc = acc1[(part, it)]
+            for g in range(g_lo, g_hi):
+                c = part * NG + g
+                nc.tensor.matmul_mx(
+                    out=acc[:],
+                    lhsT=xk[c][0][:, it * P : (it + 1) * P].bitcast(E4),
+                    lhsT_scale=xk[c][1][:, it * P : (it + 1) * P],
+                    rhs=dyk[c][0][:].bitcast(E5),
+                    rhs_scale=dyk[c][1][:],
+                    start=(g == 0),
+                    stop=(g == NG - 1),
+                )
+
+        def e1(part, it):
+            o1 = work.tile([P, D], F32, name="o1", tag="o1", bufs=4)
+            nc.scalar.copy(out=o1[:], in_=acc1.pop((part, it))[:])
+            nc.sync.dma_start(out=out_1[part, it * P : (it + 1) * P, :], in_=o1[:])
+
+        O0_SLOTS = {24: 0, 25: 1, 28: 2, 29: 3}
+        il_mid = IL_V_COLS + (D - IL_V_COLS) // 2
+        for s in range(-2, NB + 11):
+            c, r = divmod(s - 2, PACK)
+            if r == 0 and c >= 1 and c + Y_BUFS < NCH:
+                load_y(c + Y_BUFS)
+            c, r = divmod(s - 14, PACK)
+            if r == 0 and c >= 0 and c + G_BUFS < NCH:
+                load_g(c + G_BUFS)
+            c, r = divmod(s - 6, PACK)
+            if r == 0 and c >= 0 and c + X_BUFS < NCH:
+                load_x(c + X_BUFS)
+            if 0 <= s - 1 < NB:
+                pe_mt(s - 1)
+            if 0 <= s + 2 < NB:
+                pe_yt(s + 2)
+            if s == 4:
+                w_pe(0)
+            if s == 8:
+                w_pe(1)
+            c, r = divmod(s - 6, PACK)
+            if r == 0 and 0 <= c < NCH:
+                pe_e(c)
+            c, j = divmod(s - 9, PACK)
+            if 0 <= c < NCH:
+                pe_mx0(c, j)
+            if s in O0_SLOTS:
+                pe_o(0, O0_SLOTS[s], 0, NG, "wT")
+            if NB + 2 <= s < NB + 6:
+                pe_o(1, s - NB - 2, 0, NG - 1, "yT" if s - NB - 2 < 2 else "mT")
+            if s == NB + 6:
+                for it in range(PACK):
+                    pe_o(1, it, NG - 1, NG, "")
+            if 0 <= s + 1 < NB:
+                s_act(s + 1)
+            c, h = divmod(s - 4, PACK)
+            if h < 2 and 0 <= c < NCH:
+                xn(c, h)
+            c, jp = divmod(s - 6, PACK)
+            if jp < 2 and 0 <= c < NCH:
+                ev(c, jp)
+                if jp == 0:
+                    il(c, IL_V_COLS, il_mid, IL_REST)
+                else:
+                    il(c, il_mid, D, IL_REST)
+            if s == 9:
+                w_ev(1, 1, "s")
+            if s in O0_SLOTS:
+                e1(0, O0_SLOTS[s])
+            if s == NB + 6:
+                for it in range(PACK):
+                    e1(1, it)
+            if 0 <= s < NB:
+                v_bp(s)
+            c, j = divmod(s - 10, PACK)
+            if 0 <= c < NCH:
+                v_e0(c, j)
+            if 0 <= s - 2 < NB:
+                v_dy(s - 2)
+            if 0 <= s < NB:
+                v_m(s)
+            if s == 4:
+                w_ev(0, 0, "v")
+            if s == 5:
+                w_ev(0, 1, "v")
+            if s == 6:
+                w_quant(0)
+            if s == 8:
+                w_ev(1, 0, "v")
+            if s == 10:
+                w_quant(1)
+            c, r = divmod(s - 6, PACK)
+            if 0 <= c < NCH:
+                if r == 0:
+                    il(c, 0, IL_V_COLS, "v")
+                elif r == 2:
+                    v_q_dyT(c)
+                elif r == 3:
+                    v_q_dq(c)
+            c, r = divmod(s - 7, PACK)
+            if r == 0 and 0 <= c < NCH:
+                v_q_x(c)

@@ -23,11 +23,12 @@ NCH = PARTS * NG
 NB = NCH * PACK
 
 MANUAL = False
-BP_S = []
+BP_S = [1,3]
 BP_G = []
-XN_ENG = "s"
-IL_V_COLS = 192
+XN_ENG = "g"
+IL_V_COLS = 0
 IL_REST = "s"
+HP = False
 EV_ENG = "s"
 Y_BUFS = 4
 G_BUFS = 5
@@ -252,6 +253,18 @@ def tile_better_transformer_t_v_kernel(
 
         def v_dy(k):
             c, b = divmod(k, PACK)
+            if HP:
+                if b == 0:
+                    dq_t[c] = work.tile([P, D, PACK], BF16, name="dq", tag="dq", bufs=3, align_bytes=64)
+                nc.vector.scalar_tensor_tensor(
+                    out=dq_t[c][:, b * P : (b + 1) * P, :],
+                    in0=mT.pop(k)[:].rearrange("p j f -> p f j"),
+                    scalar=1.0,
+                    in1=g_t[c][:, :, b * P : (b + 1) * P].rearrange("p j f -> p f j"),
+                    op0=ALU.add,
+                    op1=ALU.mult,
+                )
+                return
             if b == 0:
                 dn_t[c] = work.tile([P, PACK, D], BF16, name="dn", tag="dn", bufs=2, align_bytes=64)
             nc.vector.scalar_tensor_tensor(
@@ -264,6 +277,15 @@ def tile_better_transformer_t_v_kernel(
             )
 
         def pe_e(c):
+            if HP:
+                words = dq_t[c][:].rearrange("p c j -> p (c j)").bitcast(F32)
+                tg_t[c] = work.tile([P, D, PACK], BF16, name="dyTg", tag="dyTg", bufs=2, align_bytes=64)
+                for v in range(2):
+                    bank = psum.tile([P, PACK, P], F32, name="d_T", tag="wT")
+                    for t in range(PACK):
+                        nc.tensor.transpose(bank[:, t, :], words[:, 2 * t + v : 2 * D : 8], ident_f[:])
+                    dT_bank[(c, v)] = bank
+                return
             words = dn_t[c][:].rearrange("p j c -> p (j c)").bitcast(F32)
             tg_t[c] = work.tile([P, D, PACK], BF16, name="dyTg", tag="dyTg", bufs=2, align_bytes=64)
             for jp in range(2):
@@ -279,6 +301,15 @@ def tile_better_transformer_t_v_kernel(
                 dT_bank[(c, jp)] = bank
 
         def ev(c, jp):
+            if HP:
+                dst = tg_t[c][:, jp * 2 * P : (jp + 1) * 2 * P, :].rearrange("q (e p) t -> q e p t", e=2)
+                src = dT_bank.pop((c, jp))[:].rearrange("q t p -> q (t p)").bitcast(BF16)
+                src = src.rearrange("q (t p e) -> q e p t", t=PACK, e=2)
+                if EV_ENG == "s":
+                    nc.scalar.copy(out=dst, in_=src)
+                else:
+                    nc.vector.tensor_copy(out=dst, in_=src)
+                return
             words_out(tg_t[c][:, jp * 2 * P : (jp + 1) * 2 * P, :], dT_bank.pop((c, jp))[:], EV_ENG)
 
         def v_q_dyT(c):
@@ -290,6 +321,8 @@ def tile_better_transformer_t_v_kernel(
             dyT[c] = (tcod, tsc)
 
         def il(c, lo, hi, eng):
+            if HP:
+                return
             if c not in dq_t:
                 dq_t[c] = work.tile([P, D, PACK], BF16, name="dq", tag="dq", bufs=2, align_bytes=64)
             if hi > lo:

@@ -9,6 +9,7 @@ F32 = mybir.dt.float32
 BF16 = mybir.dt.bfloat16
 U32 = mybir.dt.uint32
 U8 = mybir.dt.uint8
+I32 = mybir.dt.int32
 E4 = mybir.dt.float8_e4m3fn_x4
 E5 = mybir.dt.float8_e5m2_x4
 ACT = mybir.ActivationFunctionType
@@ -23,12 +24,15 @@ NCH = PARTS * NG
 NB = NCH * PACK
 
 MANUAL = False
-BP_S = [1,3]
+BP_S = []
 BP_G = []
-XN_ENG = "g"
-IL_V_COLS = 0
+XN_ENG = "s"
+IL_V_COLS = 192
 IL_REST = "s"
 HP = False
+MX0_REPEAT = 3
+WARM_HEAD = 5
+WARM_RAMP = 1
 EV_ENG = "s"
 Y_BUFS = 4
 G_BUFS = 5
@@ -110,6 +114,32 @@ def tile_better_transformer_t_v_kernel(
         nc.scalar.dma_start(out=nb_b[:], in_=norm_bias.partition_broadcast(P))
         junk2 = const.tile([P, 1], F32, name="junk2")
         nc.scalar.activation(out=junk2[:], in_=junk[:], func=ACT.Silu)
+
+        z5c = const.tile([P, P], U32, name="z5c", align_bytes=64)
+        z5s = const.tile([P, P], U8, name="z5s", align_bytes=64)
+        z4c = const.tile([P, D], U32, name="z4c", align_bytes=64)
+        z4s = const.tile([P, D], U8, name="z4s", align_bytes=64)
+        if WARM_HEAD + WARM_RAMP > 0:
+            zb = const.tile([P, PACK * D], BF16, name="zb", align_bytes=64)
+            nc.vector.memset(zb[:], 0.0)
+            nc.vector.quantize_mx(out=z5c[:].bitcast(E5), scales=z5s[:], in_=zb[:, 0 : PACK * P])
+            nc.vector.quantize_mx(out=z4c[:].bitcast(E4), scales=z4s[:], in_=zb[:])
+
+        def warm(n):
+            if n > 0:
+                scratch = psum.tile([P, D], F32, name="warm", tag="acc")
+                for i in range(n):
+                    nc.tensor.matmul_mx(
+                        out=scratch[:],
+                        lhsT=z5c[:].bitcast(E5),
+                        lhsT_scale=z5s[:],
+                        rhs=z4c[:].bitcast(E4),
+                        rhs_scale=z4s[:],
+                        start=True,
+                        stop=True,
+                    )
+
+        warm(WARM_HEAD)
 
         load_y0()
         load_g(0)
@@ -340,15 +370,16 @@ def tile_better_transformer_t_v_kernel(
             part = c // NG
             tcod, tsc = dyT[c]
             acc = psum.tile([P, D], F32, name="acc0", tag="acc")
-            nc.tensor.matmul_mx(
-                out=acc[:],
-                lhsT=tcod[:, j * P : (j + 1) * P].bitcast(E5),
-                lhsT_scale=tsc[:, j * P : (j + 1) * P],
-                rhs=w_q[part][0][:].bitcast(E4),
-                rhs_scale=w_q[part][1][:],
-                start=True,
-                stop=True,
-            )
+            for rep in range(MX0_REPEAT):
+                nc.tensor.matmul_mx(
+                    out=acc[:],
+                    lhsT=tcod[:, j * P : (j + 1) * P].bitcast(E5),
+                    lhsT_scale=tsc[:, j * P : (j + 1) * P],
+                    rhs=w_q[part][0][:].bitcast(E4),
+                    rhs_scale=w_q[part][1][:],
+                    start=True,
+                    stop=True,
+                )
             acc0[(c, j)] = acc
 
         def v_e0(c, j):
@@ -424,6 +455,8 @@ def tile_better_transformer_t_v_kernel(
                 pe_mt(s - 1)
             if 0 <= s + 2 < NB:
                 pe_yt(s + 2)
+            if s < 9:
+                warm(WARM_RAMP)
             if s == 4:
                 w_pe(0)
             if s == 8:

@@ -9,7 +9,6 @@ F32 = mybir.dt.float32
 BF16 = mybir.dt.bfloat16
 U32 = mybir.dt.uint32
 U8 = mybir.dt.uint8
-I32 = mybir.dt.int32
 E4 = mybir.dt.float8_e4m3fn_x4
 E5 = mybir.dt.float8_e5m2_x4
 ACT = mybir.ActivationFunctionType
@@ -24,19 +23,27 @@ NCH = PARTS * NG
 NB = NCH * PACK
 
 MANUAL = False
+HP = True
 BP_S = []
-BP_G = []
-XN_ENG = "s"
 IL_V_COLS = 192
-IL_REST = "s"
-HP = False
-MX0_REPEAT = 3
-WARM_HEAD = 5
-WARM_RAMP = 1
-EV_ENG = "s"
 Y_BUFS = 4
 G_BUFS = 5
 X_BUFS = 3
+L_YT = 2
+L_ACT = 1
+L_MT = 1
+L_DY = 2
+S_E = 6
+S_QT = 8
+S_QK = 6
+S_MX = 9
+S_E0 = 10
+S_XN = 4
+S_QX = 7
+S_W = (4, 8)
+O0_SLOTS = (24, 25, 28, 29)
+O1_START = 34
+O1_FIN = 38
 
 
 def tile_better_transformer_t_v_kernel(
@@ -62,25 +69,27 @@ def tile_better_transformer_t_v_kernel(
         y_t = {}
         g_t = {}
         x_t = {}
+        w_raw = {}
 
         def cols(part):
             return slice(part * D, (part + 1) * D)
 
-        def load_y0():
-            for b in range(PACK):
-                t = raw.tile([P, PACK, P], F32, name="y_first", tag="y0", bufs=PACK)
-                nc.sync.dma_start(out=t[:], in_=y_v[:, 0, :, b * P : (b + 1) * P])
-                y_t[(0, b)] = t
-
         def load_y(c):
             part, g = divmod(c, NG)
-            t = raw.tile([P, PACK, D], F32, name="y_raw", tag="y", bufs=Y_BUFS)
-            nc.sync.dma_start(out=t[:], in_=y_v[:, g, :, cols(part)])
-            y_t[c] = t
+            if c == 0:
+                y_t[0] = []
+                for b in range(PACK):
+                    t = raw.tile([P, PACK, P], F32, name="y_first", tag="y0", bufs=PACK)
+                    nc.sync.dma_start(out=t[:], in_=y_v[:, 0, :, b * P : (b + 1) * P])
+                    y_t[0].append(t)
+            else:
+                t = raw.tile([P, PACK, D], F32, name="y_raw", tag="y", bufs=Y_BUFS)
+                nc.sync.dma_start(out=t[:], in_=y_v[:, g, :, cols(part)])
+                y_t[c] = t
 
         def y_block(c, b, j):
             if c == 0:
-                return y_t[(0, b)][:, j, :]
+                return y_t[0][b][:, j, :]
             return y_t[c][:, j, b * P : (b + 1) * P]
 
         def load_g(c):
@@ -95,12 +104,10 @@ def tile_better_transformer_t_v_kernel(
             nc.sync.dma_start(out=t[:], in_=x_v[:, g, :, cols(part)])
             x_t[c] = t
 
-        w_raw = []
-
         def load_w(part):
             t = const.tile([P, PACK, D], BF16, name="w_raw%d" % part)
             nc.sync.dma_start(out=t[:], in_=w_v[:, part, :, :])
-            w_raw.append(t)
+            w_raw[part] = t
 
         junk = const.tile([P, 1], F32, name="junk")
         nc.vector.memset(junk[:], 0.0)
@@ -115,33 +122,7 @@ def tile_better_transformer_t_v_kernel(
         junk2 = const.tile([P, 1], F32, name="junk2")
         nc.scalar.activation(out=junk2[:], in_=junk[:], func=ACT.Silu)
 
-        z5c = const.tile([P, P], U32, name="z5c", align_bytes=64)
-        z5s = const.tile([P, P], U8, name="z5s", align_bytes=64)
-        z4c = const.tile([P, D], U32, name="z4c", align_bytes=64)
-        z4s = const.tile([P, D], U8, name="z4s", align_bytes=64)
-        if WARM_HEAD + WARM_RAMP > 0:
-            zb = const.tile([P, PACK * D], BF16, name="zb", align_bytes=64)
-            nc.vector.memset(zb[:], 0.0)
-            nc.vector.quantize_mx(out=z5c[:].bitcast(E5), scales=z5s[:], in_=zb[:, 0 : PACK * P])
-            nc.vector.quantize_mx(out=z4c[:].bitcast(E4), scales=z4s[:], in_=zb[:])
-
-        def warm(n):
-            if n > 0:
-                scratch = psum.tile([P, D], F32, name="warm", tag="acc")
-                for i in range(n):
-                    nc.tensor.matmul_mx(
-                        out=scratch[:],
-                        lhsT=z5c[:].bitcast(E5),
-                        lhsT_scale=z5s[:],
-                        rhs=z4c[:].bitcast(E4),
-                        rhs_scale=z4s[:],
-                        start=True,
-                        stop=True,
-                    )
-
-        warm(WARM_HEAD)
-
-        load_y0()
+        load_y(0)
         load_g(0)
         load_y(1)
         load_w(0)
@@ -189,14 +170,6 @@ def tile_better_transformer_t_v_kernel(
             else:
                 nc.vector.tensor_copy(out=dw, in_=src)
 
-        def interleave(dst, src, eng):
-            if eng == "v":
-                nc.vector.tensor_copy(out=dst, in_=src)
-            elif eng == "s":
-                nc.scalar.copy(out=dst, in_=src)
-            else:
-                nc.gpsimd.tensor_scalar(out=dst, in0=src, scalar1=1.0, scalar2=0.0, op0=ALU.mult, op1=ALU.add)
-
         w_bank = {}
         w_g = {}
         w_q = {}
@@ -235,6 +208,10 @@ def tile_better_transformer_t_v_kernel(
         xk = {}
         dyT = {}
         acc0 = {}
+        acc1 = {}
+
+        def vcol(k):
+            return (k // (PACK * NG)) * PACK + k % PACK
 
         def pe_yt(k):
             c, b = divmod(k, PACK)
@@ -244,27 +221,23 @@ def tile_better_transformer_t_v_kernel(
             yT[k] = bank
 
         def s_act(k):
+            col = vcol(k)
             flat = yT.pop(k)[:].rearrange("p j t -> p (j t)")
-            th = work.tile([P, D], F32, name="th", tag="th", bufs=5)
-            col = (k // PACK // NG) * PACK + k % PACK
-            nc.scalar.activation(out=th[:], in_=flat, func=ACT.Tanh, scale=hbe[:, col : col + 1])
             s1 = work.tile([P, D], F32, name="s1", tag="s1", bufs=4)
             nc.scalar.activation(out=s1[:], in_=flat, func=ACT.Silu, scale=be[:, col : col + 1])
+            th = work.tile([P, D], F32, name="th", tag="th", bufs=5)
+            nc.scalar.activation(out=th[:], in_=flat, func=ACT.Tanh, scale=hbe[:, col : col + 1])
             if k % PACK in BP_S:
                 nc.scalar.activation(
                     out=s1[:], in_=s1[:], func=ACT.Identity, scale=cneg[:, col : col + 1], bias=mcneg[:, col : col + 1]
-                )
-            elif k % PACK in BP_G:
-                nc.gpsimd.tensor_scalar(
-                    out=s1[:], in0=s1[:], scalar1=-1.0, scalar2=cneg[:, col : col + 1], op0=ALU.add, op1=ALU.mult
                 )
             th_t[k] = th
             s1_t[k] = s1
 
         def v_bp(k):
-            col = (k // PACK // NG) * PACK + k % PACK
+            col = vcol(k)
             s1 = s1_t[k]
-            if k % PACK not in BP_S and k % PACK not in BP_G:
+            if k % PACK not in BP_S:
                 nc.vector.tensor_scalar(
                     out=s1[:], in0=s1[:], scalar1=-1.0, scalar2=cneg[:, col : col + 1], op0=ALU.add, op1=ALU.mult
                 )
@@ -307,9 +280,9 @@ def tile_better_transformer_t_v_kernel(
             )
 
         def pe_e(c):
+            tg_t[c] = work.tile([P, D, PACK], BF16, name="dyTg", tag="dyTg", bufs=2, align_bytes=64)
             if HP:
                 words = dq_t[c][:].rearrange("p c j -> p (c j)").bitcast(F32)
-                tg_t[c] = work.tile([P, D, PACK], BF16, name="dyTg", tag="dyTg", bufs=2, align_bytes=64)
                 for v in range(2):
                     bank = psum.tile([P, PACK, P], F32, name="d_T", tag="wT")
                     for t in range(PACK):
@@ -317,7 +290,6 @@ def tile_better_transformer_t_v_kernel(
                     dT_bank[(c, v)] = bank
                 return
             words = dn_t[c][:].rearrange("p j c -> p (j c)").bitcast(F32)
-            tg_t[c] = work.tile([P, D, PACK], BF16, name="dyTg", tag="dyTg", bufs=2, align_bytes=64)
             for jp in range(2):
                 bank = psum.tile([P, 2, 2 * P], F32, name="d_T", tag="wT")
                 for u in range(2):
@@ -330,17 +302,17 @@ def tile_better_transformer_t_v_kernel(
                         )
                 dT_bank[(c, jp)] = bank
 
-        def ev(c, jp):
+        def ev(c, jp, eng):
             if HP:
                 dst = tg_t[c][:, jp * 2 * P : (jp + 1) * 2 * P, :].rearrange("q (e p) t -> q e p t", e=2)
                 src = dT_bank.pop((c, jp))[:].rearrange("q t p -> q (t p)").bitcast(BF16)
                 src = src.rearrange("q (t p e) -> q e p t", t=PACK, e=2)
-                if EV_ENG == "s":
+                if eng == "s":
                     nc.scalar.copy(out=dst, in_=src)
                 else:
                     nc.vector.tensor_copy(out=dst, in_=src)
                 return
-            words_out(tg_t[c][:, jp * 2 * P : (jp + 1) * 2 * P, :], dT_bank.pop((c, jp))[:], EV_ENG)
+            words_out(tg_t[c][:, jp * 2 * P : (jp + 1) * 2 * P, :], dT_bank.pop((c, jp))[:], eng)
 
         def v_q_dyT(c):
             tcod = work.tile([P, D], U32, name="dyT_codes", tag="dyTc", bufs=2, align_bytes=64)
@@ -356,7 +328,12 @@ def tile_better_transformer_t_v_kernel(
             if c not in dq_t:
                 dq_t[c] = work.tile([P, D, PACK], BF16, name="dq", tag="dq", bufs=2, align_bytes=64)
             if hi > lo:
-                interleave(dq_t[c][:, lo:hi, :], dn_t[c][:, :, lo:hi].rearrange("p j c -> p c j"), eng)
+                dst = dq_t[c][:, lo:hi, :]
+                src = dn_t[c][:, :, lo:hi].rearrange("p j c -> p c j")
+                if eng == "v":
+                    nc.vector.tensor_copy(out=dst, in_=src)
+                else:
+                    nc.scalar.copy(out=dst, in_=src)
 
         def v_q_dq(c):
             kc = keep.tile([P, D], U32, name="dyk_codes%d" % c, align_bytes=64)
@@ -369,17 +346,16 @@ def tile_better_transformer_t_v_kernel(
         def pe_mx0(c, j):
             part = c // NG
             tcod, tsc = dyT[c]
-            acc = psum.tile([P, D], F32, name="acc0", tag="acc")
-            for rep in range(MX0_REPEAT):
-                nc.tensor.matmul_mx(
-                    out=acc[:],
-                    lhsT=tcod[:, j * P : (j + 1) * P].bitcast(E5),
-                    lhsT_scale=tsc[:, j * P : (j + 1) * P],
-                    rhs=w_q[part][0][:].bitcast(E4),
-                    rhs_scale=w_q[part][1][:],
-                    start=True,
-                    stop=True,
-                )
+            acc = psum.tile([P, D], F32, name="acc0", tag="wT" if (c == NCH - 1 and j >= 2) else "acc")
+            nc.tensor.matmul_mx(
+                out=acc[:],
+                lhsT=tcod[:, j * P : (j + 1) * P].bitcast(E5),
+                lhsT_scale=tsc[:, j * P : (j + 1) * P],
+                rhs=w_q[part][0][:].bitcast(E4),
+                rhs_scale=w_q[part][1][:],
+                start=True,
+                stop=True,
+            )
             acc0[(c, j)] = acc
 
         def v_e0(c, j):
@@ -395,18 +371,13 @@ def tile_better_transformer_t_v_kernel(
                 xq_t[c] = work.tile([P, D, PACK], BF16, name="xq", tag="xq", bufs=2, align_bytes=64)
             lo = h * (D // 2)
             hi = lo + D // 2
-            dst = xq_t[c][:, lo:hi, :]
-            src = x_t[c][:, :, lo:hi].rearrange("p j c -> p c j")
-            if XN_ENG == "s":
-                nc.scalar.activation(out=dst, in_=src, func=ACT.Identity, scale=gain_c[:, 0:1], bias=nb_c[:, 0:1])
-            elif XN_ENG == "v":
-                nc.vector.tensor_scalar(
-                    out=dst, in0=src, scalar1=gain_c[:, 0:1], scalar2=nb_c[:, 0:1], op0=ALU.mult, op1=ALU.add
-                )
-            else:
-                nc.gpsimd.tensor_scalar(
-                    out=dst, in0=src, scalar1=gain_c[:, 0:1], scalar2=nb_c[:, 0:1], op0=ALU.mult, op1=ALU.add
-                )
+            nc.scalar.activation(
+                out=xq_t[c][:, lo:hi, :],
+                in_=x_t[c][:, :, lo:hi].rearrange("p j c -> p c j"),
+                func=ACT.Identity,
+                scale=gain_c[:, 0:1],
+                bias=nb_c[:, 0:1],
+            )
 
         def v_q_x(c):
             kc = keep.tile([P, D], U32, name="xk_codes%d" % c, align_bytes=64)
@@ -415,8 +386,6 @@ def tile_better_transformer_t_v_kernel(
                 out=kc[:].bitcast(E4), scales=ks[:], in_=xq_t.pop(c)[:].rearrange("p c j -> p (c j)")
             )
             xk[c] = (kc, ks)
-
-        acc1 = {}
 
         def pe_o(part, it, g_lo, g_hi, tag):
             if g_lo == 0:
@@ -437,89 +406,79 @@ def tile_better_transformer_t_v_kernel(
         def e1(part, it):
             o1 = work.tile([P, D], F32, name="o1", tag="o1", bufs=4)
             nc.scalar.copy(out=o1[:], in_=acc1.pop((part, it))[:])
-            nc.sync.dma_start(out=out_1[part, it * P : (it + 1) * P, :], in_=o1[:])
+            nc.scalar.dma_start(out=out_1[part, it * P : (it + 1) * P, :], in_=o1[:])
 
-        O0_SLOTS = {24: 0, 25: 1, 28: 2, 29: 3}
         il_mid = IL_V_COLS + (D - IL_V_COLS) // 2
-        for s in range(-2, NB + 11):
-            c, r = divmod(s - 2, PACK)
+        for s in range(-L_YT, NB + S_E0 + 1):
+            c, r = divmod(s + L_YT - PACK, PACK)
             if r == 0 and c >= 1 and c + Y_BUFS < NCH:
                 load_y(c + Y_BUFS)
-            c, r = divmod(s - 14, PACK)
+            c, r = divmod(s - S_E0 - PACK, PACK)
             if r == 0 and c >= 0 and c + G_BUFS < NCH:
                 load_g(c + G_BUFS)
-            c, r = divmod(s - 6, PACK)
+            c, r = divmod(s - S_XN - 2, PACK)
             if r == 0 and c >= 0 and c + X_BUFS < NCH:
                 load_x(c + X_BUFS)
-            if 0 <= s - 1 < NB:
-                pe_mt(s - 1)
-            if 0 <= s + 2 < NB:
-                pe_yt(s + 2)
-            if s < 9:
-                warm(WARM_RAMP)
-            if s == 4:
-                w_pe(0)
-            if s == 8:
-                w_pe(1)
-            c, r = divmod(s - 6, PACK)
+            if 0 <= s - L_MT < NB:
+                pe_mt(s - L_MT)
+            if 0 <= s + L_YT < NB:
+                pe_yt(s + L_YT)
+            if s in S_W:
+                w_pe(S_W.index(s))
+            c, r = divmod(s - S_E, PACK)
             if r == 0 and 0 <= c < NCH:
                 pe_e(c)
-            c, j = divmod(s - 9, PACK)
+            c, j = divmod(s - S_MX, PACK)
             if 0 <= c < NCH:
                 pe_mx0(c, j)
             if s in O0_SLOTS:
-                pe_o(0, O0_SLOTS[s], 0, NG, "wT")
-            if NB + 2 <= s < NB + 6:
-                pe_o(1, s - NB - 2, 0, NG - 1, "yT" if s - NB - 2 < 2 else "mT")
-            if s == NB + 6:
+                pe_o(0, O0_SLOTS.index(s), 0, NG, "wT")
+            if O1_START <= s < O1_START + PACK:
+                pe_o(1, s - O1_START, 0, NG - 1, "yT" if s - O1_START < 2 else "mT")
+            if s == O1_FIN:
                 for it in range(PACK):
                     pe_o(1, it, NG - 1, NG, "")
-            if 0 <= s + 1 < NB:
-                s_act(s + 1)
-            c, h = divmod(s - 4, PACK)
+            if 0 <= s + L_ACT < NB:
+                s_act(s + L_ACT)
+            c, h = divmod(s - S_XN, PACK)
             if h < 2 and 0 <= c < NCH:
                 xn(c, h)
-            c, jp = divmod(s - 6, PACK)
+            c, jp = divmod(s - S_E, PACK)
             if jp < 2 and 0 <= c < NCH:
-                ev(c, jp)
+                ev(c, jp, "s")
                 if jp == 0:
-                    il(c, IL_V_COLS, il_mid, IL_REST)
+                    il(c, IL_V_COLS, il_mid, "s")
                 else:
-                    il(c, il_mid, D, IL_REST)
-            if s == 9:
-                w_ev(1, 1, "s")
+                    il(c, il_mid, D, "s")
+            if s - 1 in S_W:
+                w_ev(S_W.index(s - 1), 1, "s")
             if s in O0_SLOTS:
-                e1(0, O0_SLOTS[s])
-            if s == NB + 6:
+                e1(0, O0_SLOTS.index(s))
+            if s == O1_FIN:
                 for it in range(PACK):
                     e1(1, it)
             if 0 <= s < NB:
                 v_bp(s)
-            c, j = divmod(s - 10, PACK)
+            c, j = divmod(s - S_E0, PACK)
             if 0 <= c < NCH:
                 v_e0(c, j)
-            if 0 <= s - 2 < NB:
-                v_dy(s - 2)
+            if 0 <= s - L_DY < NB:
+                v_dy(s - L_DY)
             if 0 <= s < NB:
                 v_m(s)
-            if s == 4:
-                w_ev(0, 0, "v")
-            if s == 5:
-                w_ev(0, 1, "v")
-            if s == 6:
-                w_quant(0)
-            if s == 8:
-                w_ev(1, 0, "v")
-            if s == 10:
-                w_quant(1)
-            c, r = divmod(s - 6, PACK)
-            if 0 <= c < NCH:
-                if r == 0:
-                    il(c, 0, IL_V_COLS, "v")
-                elif r == 2:
-                    v_q_dyT(c)
-                elif r == 3:
-                    v_q_dq(c)
-            c, r = divmod(s - 7, PACK)
+            if s in S_W:
+                w_ev(S_W.index(s), 0, "v")
+            if s - 2 in S_W:
+                w_quant(S_W.index(s - 2))
+            c, r = divmod(s - S_E, PACK)
+            if r == 0 and 0 <= c < NCH:
+                il(c, 0, IL_V_COLS, "v")
+            c, r = divmod(s - S_QT, PACK)
+            if r == 0 and 0 <= c < NCH:
+                v_q_dyT(c)
+            c, r = divmod(s - S_QK, PACK)
+            if r == 0 and 0 <= c < NCH:
+                v_q_dq(c)
+            c, r = divmod(s - S_QX, PACK)
             if r == 0 and 0 <= c < NCH:
                 v_q_x(c)

@@ -9,8 +9,8 @@ F32 = mybir.dt.float32
 BF16 = mybir.dt.bfloat16
 U32 = mybir.dt.uint32
 U8 = mybir.dt.uint8
-E4 = mybir.dt.float8_e4m3fn_x4
-E5 = mybir.dt.float8_e5m2_x4
+E4M3 = mybir.dt.float8_e4m3fn_x4
+E5M2 = mybir.dt.float8_e5m2_x4
 ACT = mybir.ActivationFunctionType
 ALU = mybir.AluOpType
 
@@ -18,32 +18,33 @@ P = 128
 PACK = 4
 D = 512
 PARTS = 2
-NG = 4
-NCH = PARTS * NG
-NB = NCH * PACK
+GROUPS = 4
+CHUNKS = PARTS * GROUPS
+BLOCKS = CHUNKS * PACK
 
-MANUAL = False
-HP = True
-BP_S = []
-IL_V_COLS = 192
 Y_BUFS = 4
 G_BUFS = 5
 X_BUFS = 3
-L_YT = 2
-L_ACT = 1
-L_MT = 1
-L_DY = 2
-S_E = 6
-S_QT = 8
-S_QK = 6
-S_MX = 9
-S_E0 = 10
-S_XN = 4
-S_QX = 7
-S_W = (4, 8)
-O0_SLOTS = (24, 25, 28, 29)
-O1_START = 34
-O1_FIN = 38
+
+LEAD_Y_TRANSPOSE = 3
+LEAD_ACTIVATION = 2
+LEAD_FACTOR = 1
+LAG_M_TRANSPOSE = 1
+LAG_DY = 2
+AT_QUANT_TOKENS = 6
+AT_DY_TRANSPOSE = 6
+AT_DY_COPY = 7
+AT_QUANT_FEATURES = 9
+AT_OUT0_MATMUL = 10
+AT_OUT0_FINISH = 11
+XN_FIRST = 9
+XN_PIECES = 5
+XN_SLOTS = 8
+XN_QUANT_LAG = 2
+AT_WEIGHTS = (4, 6)
+AT_OUT1_PART0 = (24, 25, 28, 29)
+AT_OUT1_PART1 = 34
+AT_OUT1_LAST = 38
 
 
 def tile_better_transformer_t_v_kernel(
@@ -51,76 +52,74 @@ def tile_better_transformer_t_v_kernel(
 ):
     nc = tc.nc
 
-    y_v = y.rearrange("(g p j) w -> p g j w", p=P, j=PACK)
-    g_v = grad_out.rearrange("(g p j) w -> p g j w", p=P, j=PACK)
-    x_v = x.rearrange("(g p j) w -> p g j w", p=P, j=PACK)
-    o0_v = out_0.rearrange("(g p j) w -> p g j w", p=P, j=PACK)
-    w_v = weights.rearrange("a (t p) o -> p a t o", p=P)
+    y_view = y.rearrange("(g p j) w -> p g j w", p=P, j=PACK)
+    g_view = grad_out.rearrange("(g p j) w -> p g j w", p=P, j=PACK)
+    x_view = x.rearrange("(g p j) w -> p g j w", p=P, j=PACK)
+    out0_view = out_0.rearrange("(g p j) w -> p g j w", p=P, j=PACK)
+    w_view = weights.rearrange("a (t p) o -> p a t o", p=P)
 
     with ExitStack() as ctx:
-        if MANUAL:
-            ctx.enter_context(tc.manual_schedule())
         const = ctx.enter_context(tc.tile_pool(name="const", bufs=1))
         keep = ctx.enter_context(tc.tile_pool(name="keep", bufs=1))
         raw = ctx.enter_context(tc.tile_pool(name="raw", bufs=2))
         work = ctx.enter_context(tc.tile_pool(name="work", bufs=2))
         psum = ctx.enter_context(tc.psum_pool(name="psum", bufs=2))
 
-        y_t = {}
-        g_t = {}
-        x_t = {}
+        y_raw = {}
+        g_raw = {}
+        x_raw = {}
         w_raw = {}
 
-        def cols(part):
+        def part_columns(part):
             return slice(part * D, (part + 1) * D)
 
         def load_y(c):
-            part, g = divmod(c, NG)
+            part, g = divmod(c, GROUPS)
             if c == 0:
-                y_t[0] = []
+                y_raw[0] = []
                 for b in range(PACK):
-                    t = raw.tile([P, PACK, P], F32, name="y_first", tag="y0", bufs=PACK)
-                    nc.sync.dma_start(out=t[:], in_=y_v[:, 0, :, b * P : (b + 1) * P])
-                    y_t[0].append(t)
+                    t = raw.tile([P, PACK, P], F32, name="y_first", tag="y_first", bufs=PACK)
+                    nc.sync.dma_start(out=t[:], in_=y_view[:, 0, :, b * P : (b + 1) * P])
+                    y_raw[0].append(t)
             else:
                 t = raw.tile([P, PACK, D], F32, name="y_raw", tag="y", bufs=Y_BUFS)
-                nc.sync.dma_start(out=t[:], in_=y_v[:, g, :, cols(part)])
-                y_t[c] = t
+                nc.sync.dma_start(out=t[:], in_=y_view[:, g, :, part_columns(part)])
+                y_raw[c] = t
 
         def y_block(c, b, j):
             if c == 0:
-                return y_t[0][b][:, j, :]
-            return y_t[c][:, j, b * P : (b + 1) * P]
+                return y_raw[0][b][:, j, :]
+            return y_raw[c][:, j, b * P : (b + 1) * P]
 
         def load_g(c):
-            part, g = divmod(c, NG)
+            part, g = divmod(c, GROUPS)
             t = raw.tile([P, PACK, D], BF16, name="g_raw", tag="g", bufs=G_BUFS)
-            nc.sync.dma_start(out=t[:], in_=g_v[:, g, :, cols(part)])
-            g_t[c] = t
+            nc.sync.dma_start(out=t[:], in_=g_view[:, g, :, part_columns(part)])
+            g_raw[c] = t
 
         def load_x(c):
-            part, g = divmod(c, NG)
+            part, g = divmod(c, GROUPS)
             t = raw.tile([P, PACK, D], BF16, name="x_raw", tag="x", bufs=X_BUFS)
-            nc.sync.dma_start(out=t[:], in_=x_v[:, g, :, cols(part)])
-            x_t[c] = t
+            nc.sync.dma_start(out=t[:], in_=x_view[:, g, :, part_columns(part)])
+            x_raw[c] = t
 
         def load_w(part):
             t = const.tile([P, PACK, D], BF16, name="w_raw%d" % part)
-            nc.sync.dma_start(out=t[:], in_=w_v[:, part, :, :])
+            nc.sync.dma_start(out=t[:], in_=w_view[:, part, :, :])
             w_raw[part] = t
 
-        junk = const.tile([P, 1], F32, name="junk")
-        nc.vector.memset(junk[:], 0.0)
-        vecs = const.tile([P, P], BF16, name="vecs")
-        nc.vector.memset(vecs[:], 0.0)
-        nc.scalar.dma_start(out=vecs[0:8, :], in_=beta.rearrange("(c f) -> c f", f=P))
-        nc.scalar.dma_start(out=vecs[8:16, :], in_=gamma.rearrange("(c f) -> c f", f=P))
-        gain_b = const.tile([P, 1], BF16, name="gain_b")
-        nc.scalar.dma_start(out=gain_b[:], in_=gain.partition_broadcast(P))
-        nb_b = const.tile([P, 1], BF16, name="nb_b")
-        nc.scalar.dma_start(out=nb_b[:], in_=norm_bias.partition_broadcast(P))
-        junk2 = const.tile([P, 1], F32, name="junk2")
-        nc.scalar.activation(out=junk2[:], in_=junk[:], func=ACT.Silu)
+        zero = const.tile([P, 1], F32, name="zero")
+        nc.vector.memset(zero[:], 0.0)
+        vectors = const.tile([P, P], BF16, name="vectors")
+        nc.vector.memset(vectors[:], 0.0)
+        nc.sync.dma_start(out=vectors[0:8, :], in_=beta.rearrange("(i f) -> i f", f=P))
+        nc.sync.dma_start(out=vectors[8:16, :], in_=gamma.rearrange("(i f) -> i f", f=P))
+        gain_bf = const.tile([P, 1], BF16, name="gain_bf")
+        nc.sync.dma_start(out=gain_bf[:], in_=gain.partition_broadcast(P))
+        nbias_bf = const.tile([P, 1], BF16, name="nbias_bf")
+        nc.sync.dma_start(out=nbias_bf[:], in_=norm_bias.partition_broadcast(P))
+        table_warm = const.tile([P, 1], F32, name="table_warm")
+        nc.scalar.activation(out=table_warm[:], in_=zero[:], func=ACT.Silu)
 
         load_y(0)
         load_g(0)
@@ -138,347 +137,301 @@ def tile_better_transformer_t_v_kernel(
         load_y(4)
         load_g(4)
 
-        ident_f = const.tile([P, P], F32, name="ident_f")
-        make_identity(nc, ident_f[:])
-        ident_b = const.tile([P, P], BF16, name="ident_b")
-        make_identity(nc, ident_b[:])
+        ident_f32 = const.tile([P, P], F32, name="ident_f32")
+        make_identity(nc, ident_f32[:])
+        ident_bf = const.tile([P, P], BF16, name="ident_bf")
+        make_identity(nc, ident_bf[:])
 
-        vecs_T = psum.tile([P, P], BF16, name="vecs_T", tag="wT")
-        nc.tensor.transpose(vecs_T[:], vecs[:], ident_b[:])
-        be = const.tile([P, 8], F32, name="be")
-        nc.vector.tensor_copy(out=be[:], in_=vecs_T[:, 0:8])
-        hbe = const.tile([P, 8], F32, name="hbe")
-        nc.vector.tensor_scalar(out=hbe[:], in0=vecs_T[:, 0:8], scalar1=0.5, scalar2=None, op0=ALU.mult)
-        cneg = const.tile([P, 8], F32, name="cneg")
+        vectors_T = psum.tile([P, P], BF16, name="vectors_T", tag="dT")
+        nc.tensor.transpose(vectors_T[:], vectors[:], ident_bf[:])
+        beta_col = const.tile([P, 8], F32, name="beta_col")
+        nc.vector.tensor_copy(out=beta_col[:], in_=vectors_T[:, 0:8])
+        half_beta_col = const.tile([P, 8], F32, name="half_beta_col")
         nc.vector.tensor_scalar(
-            out=cneg[:], in0=vecs_T[:, 8:16], scalar1=-1.0, scalar2=0.5, op0=ALU.add, op1=ALU.mult
+            out=half_beta_col[:], in0=vectors_T[:, 0:8], scalar1=0.5, scalar2=None, op0=ALU.mult
         )
-        mcneg = const.tile([P, 8], F32, name="mcneg")
+        factor_col = const.tile([P, 8], F32, name="factor_col")
         nc.vector.tensor_scalar(
-            out=mcneg[:], in0=vecs_T[:, 8:16], scalar1=-1.0, scalar2=-0.5, op0=ALU.add, op1=ALU.mult
+            out=factor_col[:], in0=vectors_T[:, 8:16], scalar1=-1.0, scalar2=0.5, op0=ALU.add, op1=ALU.mult
         )
-        gain_c = const.tile([P, 1], F32, name="gain_c")
-        nc.vector.tensor_copy(out=gain_c[:], in_=gain_b[:])
-        nb_c = const.tile([P, 1], F32, name="nb_c")
-        nc.vector.tensor_copy(out=nb_c[:], in_=nb_b[:])
-
-        def words_out(dst, bank, eng):
-            dw = dst.rearrange("p r t -> p (r t)").bitcast(F32).rearrange("p (r u) -> p r u", u=2)
-            src = bank.rearrange("p u r -> p r u")
-            if eng == "s":
-                nc.scalar.copy(out=dw, in_=src)
-            else:
-                nc.vector.tensor_copy(out=dw, in_=src)
+        gain_col = const.tile([P, 1], F32, name="gain_col")
+        nc.vector.tensor_copy(out=gain_col[:], in_=gain_bf[:])
+        nbias_col = const.tile([P, 1], F32, name="nbias_col")
+        nc.vector.tensor_copy(out=nbias_col[:], in_=nbias_bf[:])
 
         w_bank = {}
-        w_g = {}
-        w_q = {}
+        w_grouped = {}
+        w_mx = {}
 
-        def w_pe(part):
-            w_g[part] = work.tile([P, D, PACK], BF16, name="wg", tag="wg", bufs=2, align_bytes=64)
+        def transpose_weights(part):
+            w_grouped[part] = work.tile([P, D, PACK], BF16, name="w_grouped", tag="w_grouped", bufs=2, align_bytes=64)
             for h in range(2):
-                bank = psum.tile([P, 2, 2 * P], F32, name="w_T", tag="wT")
+                bank = psum.tile([P, 2, 2 * P], F32, name="w_T", tag="dT" if part == 0 else "acc")
                 for u in range(2):
-                    for t2 in range(2):
-                        ww = w_raw[part][:, 2 * h + t2, :].bitcast(F32)
-                        nc.tensor.transpose(bank[:, u, t2 * P : (t2 + 1) * P], ww[:, u : D // 2 : 2], ident_f[:])
+                    for t in range(2):
+                        words = w_raw[part][:, 2 * h + t, :].bitcast(F32)
+                        nc.tensor.transpose(bank[:, u, t * P : (t + 1) * P], words[:, u : D // 2 : 2], ident_f32[:])
                 w_bank[(part, h)] = bank
 
-        def w_ev(part, h, eng):
-            words_out(w_g[part][:, h * 2 * P : (h + 1) * 2 * P, :], w_bank.pop((part, h))[:], eng)
+        def copy_weights(part, h, engine):
+            dst = w_grouped[part][:, h * 2 * P : (h + 1) * 2 * P, :]
+            dst = dst.rearrange("q i t -> q (i t)").bitcast(F32).rearrange("q (i u) -> q i u", u=2)
+            src = w_bank.pop((part, h))[:].rearrange("q u i -> q i u")
+            if engine == "scalar":
+                nc.scalar.copy(out=dst, in_=src)
+            else:
+                nc.vector.tensor_copy(out=dst, in_=src)
 
-        def w_quant(part):
-            wc = keep.tile([P, D], U32, name="w_codes%d" % part, align_bytes=64)
-            ws = keep.tile([P, D], U8, name="w_scales%d" % part, align_bytes=64)
+        def quantize_weights(part):
+            codes = keep.tile([P, D], U32, name="w_codes%d" % part, align_bytes=64)
+            scales = keep.tile([P, D], U8, name="w_scales%d" % part, align_bytes=64)
             nc.vector.quantize_mx(
-                out=wc[:].bitcast(E4), scales=ws[:], in_=w_g[part][:].rearrange("p r t -> p (r t)")
+                out=codes[:].bitcast(E4M3), scales=scales[:], in_=w_grouped[part][:].rearrange("q i t -> q (i t)")
             )
-            w_q[part] = (wc, ws)
+            w_mx[part] = (codes, scales)
 
-        yT = {}
-        th_t = {}
-        s1_t = {}
-        mT = {}
-        dn_t = {}
-        dq_t = {}
-        tg_t = {}
-        dT_bank = {}
-        dyk = {}
-        xq_t = {}
-        xk = {}
-        dyT = {}
-        acc0 = {}
-        acc1 = {}
+        y_bank = {}
+        tanh_tile = {}
+        silu_tile = {}
+        m_bank = {}
+        dy_tile = {}
 
-        def vcol(k):
-            return (k // (PACK * NG)) * PACK + k % PACK
+        def vector_column(k):
+            return (k // (PACK * GROUPS)) * PACK + k % PACK
 
-        def pe_yt(k):
+        def transpose_y(k):
             c, b = divmod(k, PACK)
             bank = psum.tile([P, PACK, P], F32, name="y_T", tag="yT")
             for j in range(PACK):
-                nc.tensor.transpose(bank[:, j, :], y_block(c, b, j), ident_f[:])
-            yT[k] = bank
+                nc.tensor.transpose(bank[:, j, :], y_block(c, b, j), ident_f32[:])
+            y_bank[k] = bank
 
-        def s_act(k):
-            col = vcol(k)
-            flat = yT.pop(k)[:].rearrange("p j t -> p (j t)")
-            s1 = work.tile([P, D], F32, name="s1", tag="s1", bufs=4)
-            nc.scalar.activation(out=s1[:], in_=flat, func=ACT.Silu, scale=be[:, col : col + 1])
-            th = work.tile([P, D], F32, name="th", tag="th", bufs=5)
-            nc.scalar.activation(out=th[:], in_=flat, func=ACT.Tanh, scale=hbe[:, col : col + 1])
-            if k % PACK in BP_S:
-                nc.scalar.activation(
-                    out=s1[:], in_=s1[:], func=ACT.Identity, scale=cneg[:, col : col + 1], bias=mcneg[:, col : col + 1]
-                )
-            th_t[k] = th
-            s1_t[k] = s1
+        def activations(k):
+            i = vector_column(k)
+            yT = y_bank.pop(k)[:].rearrange("f j p -> f (j p)")
+            s = work.tile([P, D], F32, name="silu", tag="silu", bufs=5)
+            nc.scalar.activation(out=s[:], in_=yT, func=ACT.Silu, scale=beta_col[:, i : i + 1])
+            t = work.tile([P, D], F32, name="tanh", tag="tanh", bufs=6)
+            nc.scalar.activation(out=t[:], in_=yT, func=ACT.Tanh, scale=half_beta_col[:, i : i + 1])
+            silu_tile[k] = s
+            tanh_tile[k] = t
 
-        def v_bp(k):
-            col = vcol(k)
-            s1 = s1_t[k]
-            if k % PACK not in BP_S:
-                nc.vector.tensor_scalar(
-                    out=s1[:], in0=s1[:], scalar1=-1.0, scalar2=cneg[:, col : col + 1], op0=ALU.add, op1=ALU.mult
-                )
+        def factor(k):
+            i = vector_column(k)
+            s = silu_tile[k]
+            nc.vector.tensor_scalar(
+                out=s[:], in0=s[:], scalar1=-1.0, scalar2=factor_col[:, i : i + 1], op0=ALU.add, op1=ALU.mult
+            )
 
-        def v_m(k):
-            th = th_t[k]
-            s1 = s1_t.pop(k)
-            nc.vector.scalar_tensor_tensor(out=th[:], in0=th[:], scalar=-1.0, in1=s1[:], op0=ALU.add, op1=ALU.mult)
-
-        def pe_mt(k):
-            bank = psum.tile([P, PACK, P], F32, name="m_T", tag="mT")
-            th = th_t.pop(k)
-            for j in range(PACK):
-                nc.tensor.transpose(bank[:, j, :], th[:, j * P : (j + 1) * P], ident_f[:])
-            mT[k] = bank
-
-        def v_dy(k):
-            c, b = divmod(k, PACK)
-            if HP:
-                if b == 0:
-                    dq_t[c] = work.tile([P, D, PACK], BF16, name="dq", tag="dq", bufs=3, align_bytes=64)
-                nc.vector.scalar_tensor_tensor(
-                    out=dq_t[c][:, b * P : (b + 1) * P, :],
-                    in0=mT.pop(k)[:].rearrange("p j f -> p f j"),
-                    scalar=1.0,
-                    in1=g_t[c][:, :, b * P : (b + 1) * P].rearrange("p j f -> p f j"),
-                    op0=ALU.add,
-                    op1=ALU.mult,
-                )
-                return
-            if b == 0:
-                dn_t[c] = work.tile([P, PACK, D], BF16, name="dn", tag="dn", bufs=2, align_bytes=64)
+        def make_m(k):
+            t = tanh_tile[k]
             nc.vector.scalar_tensor_tensor(
-                out=dn_t[c][:, :, b * P : (b + 1) * P],
-                in0=mT.pop(k)[:],
+                out=t[:], in0=t[:], scalar=-1.0, in1=silu_tile.pop(k)[:], op0=ALU.add, op1=ALU.mult
+            )
+
+        def transpose_m(k):
+            bank = psum.tile([P, PACK, P], F32, name="m_T", tag="mT")
+            m = tanh_tile.pop(k)
+            for j in range(PACK):
+                nc.tensor.transpose(bank[:, j, :], m[:, j * P : (j + 1) * P], ident_f32[:])
+            m_bank[k] = bank
+
+        def make_dy(k):
+            c, b = divmod(k, PACK)
+            if b == 0:
+                dy_tile[c] = work.tile([P, D, PACK], BF16, name="dy", tag="dy", bufs=3, align_bytes=64)
+            nc.vector.scalar_tensor_tensor(
+                out=dy_tile[c][:, b * P : (b + 1) * P, :],
+                in0=m_bank.pop(k)[:].rearrange("p j f -> p f j"),
                 scalar=1.0,
-                in1=g_t[c][:, :, b * P : (b + 1) * P],
+                in1=g_raw[c][:, :, b * P : (b + 1) * P].rearrange("p j f -> p f j"),
                 op0=ALU.add,
                 op1=ALU.mult,
             )
 
-        def pe_e(c):
-            tg_t[c] = work.tile([P, D, PACK], BF16, name="dyTg", tag="dyTg", bufs=2, align_bytes=64)
-            if HP:
-                words = dq_t[c][:].rearrange("p c j -> p (c j)").bitcast(F32)
-                for v in range(2):
-                    bank = psum.tile([P, PACK, P], F32, name="d_T", tag="wT")
-                    for t in range(PACK):
-                        nc.tensor.transpose(bank[:, t, :], words[:, 2 * t + v : 2 * D : 8], ident_f[:])
-                    dT_bank[(c, v)] = bank
-                return
-            words = dn_t[c][:].rearrange("p j c -> p (j c)").bitcast(F32)
-            for jp in range(2):
-                bank = psum.tile([P, 2, 2 * P], F32, name="d_T", tag="wT")
-                for u in range(2):
-                    for j2 in range(2):
-                        j = 2 * jp + j2
-                        nc.tensor.transpose(
-                            bank[:, u, j2 * P : (j2 + 1) * P],
-                            words[:, j * (D // 2) + u : (j + 1) * (D // 2) : 2],
-                            ident_f[:],
-                        )
-                dT_bank[(c, jp)] = bank
+        dyT_bank = {}
+        dyT_grouped = {}
+        dyT_mx = {}
+        dy_mx = {}
+        xn_tile = {}
+        xn_mx = {}
+        out0_bank = {}
+        out1_bank = {}
 
-        def ev(c, jp, eng):
-            if HP:
-                dst = tg_t[c][:, jp * 2 * P : (jp + 1) * 2 * P, :].rearrange("q (e p) t -> q e p t", e=2)
-                src = dT_bank.pop((c, jp))[:].rearrange("q t p -> q (t p)").bitcast(BF16)
-                src = src.rearrange("q (t p e) -> q e p t", t=PACK, e=2)
-                if eng == "s":
-                    nc.scalar.copy(out=dst, in_=src)
-                else:
-                    nc.vector.tensor_copy(out=dst, in_=src)
-                return
-            words_out(tg_t[c][:, jp * 2 * P : (jp + 1) * 2 * P, :], dT_bank.pop((c, jp))[:], eng)
+        def transpose_dy(c):
+            words = dy_tile[c][:].rearrange("p f j -> p (f j)").bitcast(F32)
+            dyT_grouped[c] = work.tile([P, D, PACK], BF16, name="dyT_grouped", tag="dyT_grouped", bufs=2, align_bytes=64)
+            for v in range(2):
+                bank = psum.tile([P, PACK, P], F32, name="dy_T", tag="dT")
+                for t in range(PACK):
+                    nc.tensor.transpose(bank[:, t, :], words[:, 2 * t + v : 2 * D : 2 * PACK], ident_f32[:])
+                dyT_bank[(c, v)] = bank
 
-        def v_q_dyT(c):
-            tcod = work.tile([P, D], U32, name="dyT_codes", tag="dyTc", bufs=2, align_bytes=64)
-            tsc = work.tile([P, D], U8, name="dyT_scales", tag="dyTs", bufs=2, align_bytes=64)
+        def copy_dyT(c, v):
+            dst = dyT_grouped[c][:, v * 2 * P : (v + 1) * 2 * P, :].rearrange("q (e p) t -> q e p t", e=2)
+            src = dyT_bank.pop((c, v))[:].rearrange("q t p -> q (t p)").bitcast(BF16)
+            nc.scalar.copy(out=dst, in_=src.rearrange("q (t p e) -> q e p t", t=PACK, e=2))
+
+        def quantize_dy_features(c):
+            codes = work.tile([P, D], U32, name="dyT_codes", tag="dyT_codes", bufs=2, align_bytes=64)
+            scales = work.tile([P, D], U8, name="dyT_scales", tag="dyT_scales", bufs=2, align_bytes=64)
             nc.vector.quantize_mx(
-                out=tcod[:].bitcast(E5), scales=tsc[:], in_=tg_t.pop(c)[:].rearrange("p r t -> p (r t)")
+                out=codes[:].bitcast(E5M2),
+                scales=scales[:],
+                in_=dyT_grouped.pop(c)[:].rearrange("q r t -> q (r t)"),
             )
-            dyT[c] = (tcod, tsc)
+            dyT_mx[c] = (codes, scales)
 
-        def il(c, lo, hi, eng):
-            if HP:
-                return
-            if c not in dq_t:
-                dq_t[c] = work.tile([P, D, PACK], BF16, name="dq", tag="dq", bufs=2, align_bytes=64)
-            if hi > lo:
-                dst = dq_t[c][:, lo:hi, :]
-                src = dn_t[c][:, :, lo:hi].rearrange("p j c -> p c j")
-                if eng == "v":
-                    nc.vector.tensor_copy(out=dst, in_=src)
-                else:
-                    nc.scalar.copy(out=dst, in_=src)
-
-        def v_q_dq(c):
-            kc = keep.tile([P, D], U32, name="dyk_codes%d" % c, align_bytes=64)
-            ks = keep.tile([P, D], U8, name="dyk_scales%d" % c, align_bytes=64)
+        def quantize_dy_tokens(c):
+            codes = keep.tile([P, D], U32, name="dy_codes%d" % c, align_bytes=64)
+            scales = keep.tile([P, D], U8, name="dy_scales%d" % c, align_bytes=64)
             nc.vector.quantize_mx(
-                out=kc[:].bitcast(E5), scales=ks[:], in_=dq_t.pop(c)[:].rearrange("p c j -> p (c j)")
+                out=codes[:].bitcast(E5M2), scales=scales[:], in_=dy_tile[c][:].rearrange("p f j -> p (f j)")
             )
-            dyk[c] = (kc, ks)
+            dy_mx[c] = (codes, scales)
 
-        def pe_mx0(c, j):
-            part = c // NG
-            tcod, tsc = dyT[c]
-            acc = psum.tile([P, D], F32, name="acc0", tag="wT" if (c == NCH - 1 and j >= 2) else "acc")
+        def out0_matmul(c, j):
+            part = c // GROUPS
+            codes, scales = dyT_mx[c]
+            bank = psum.tile([P, D], F32, name="out0_acc", tag="dT" if (c == CHUNKS - 1 and j >= 2) else "acc")
             nc.tensor.matmul_mx(
-                out=acc[:],
-                lhsT=tcod[:, j * P : (j + 1) * P].bitcast(E5),
-                lhsT_scale=tsc[:, j * P : (j + 1) * P],
-                rhs=w_q[part][0][:].bitcast(E4),
-                rhs_scale=w_q[part][1][:],
+                out=bank[:],
+                lhsT=codes[:, j * P : (j + 1) * P].bitcast(E5M2),
+                lhsT_scale=scales[:, j * P : (j + 1) * P],
+                rhs=w_mx[part][0][:].bitcast(E4M3),
+                rhs_scale=w_mx[part][1][:],
                 start=True,
                 stop=True,
             )
-            acc0[(c, j)] = acc
+            out0_bank[(c, j)] = bank
 
-        def v_e0(c, j):
-            part, g = divmod(c, NG)
-            o0 = work.tile([P, D], F32, name="o0", tag="o0", bufs=6)
+        def out0_finish(c, j):
+            part, g = divmod(c, GROUPS)
+            result = work.tile([P, D], F32, name="out0_rows", tag="out0_rows", bufs=6)
             nc.vector.scalar_tensor_tensor(
-                out=o0[:], in0=acc0.pop((c, j))[:], scalar=gain_c[:, 0:1], in1=g_t[c][:, j, :], op0=ALU.mult, op1=ALU.add
+                out=result[:],
+                in0=out0_bank.pop((c, j))[:],
+                scalar=gain_col[:, 0:1],
+                in1=g_raw[c][:, j, :],
+                op0=ALU.mult,
+                op1=ALU.add,
             )
-            nc.sync.dma_start(out=o0_v[:, g, j, cols(part)], in_=o0[:])
+            nc.sync.dma_start(out=out0_view[:, g, j, part_columns(part)], in_=result[:])
 
-        def xn(c, h):
-            if h == 0:
-                xq_t[c] = work.tile([P, D, PACK], BF16, name="xq", tag="xq", bufs=2, align_bytes=64)
-            lo = h * (D // 2)
+        def make_x_norm(c, half):
+            if half == 0:
+                xn_tile[c] = work.tile([P, D, PACK], BF16, name="x_norm", tag="x_norm", bufs=2, align_bytes=64)
+            lo = half * (D // 2)
             hi = lo + D // 2
             nc.scalar.activation(
-                out=xq_t[c][:, lo:hi, :],
-                in_=x_t[c][:, :, lo:hi].rearrange("p j c -> p c j"),
+                out=xn_tile[c][:, lo:hi, :],
+                in_=x_raw[c][:, :, lo:hi].rearrange("p j f -> p f j"),
                 func=ACT.Identity,
-                scale=gain_c[:, 0:1],
-                bias=nb_c[:, 0:1],
+                scale=gain_col[:, 0:1],
+                bias=nbias_col[:, 0:1],
             )
 
-        def v_q_x(c):
-            kc = keep.tile([P, D], U32, name="xk_codes%d" % c, align_bytes=64)
-            ks = keep.tile([P, D], U8, name="xk_scales%d" % c, align_bytes=64)
+        def quantize_x_norm(c):
+            codes = keep.tile([P, D], U32, name="xn_codes%d" % c, align_bytes=64)
+            scales = keep.tile([P, D], U8, name="xn_scales%d" % c, align_bytes=64)
             nc.vector.quantize_mx(
-                out=kc[:].bitcast(E4), scales=ks[:], in_=xq_t.pop(c)[:].rearrange("p c j -> p (c j)")
+                out=codes[:].bitcast(E4M3), scales=scales[:], in_=xn_tile.pop(c)[:].rearrange("p f j -> p (f j)")
             )
-            xk[c] = (kc, ks)
+            xn_mx[c] = (codes, scales)
 
-        def pe_o(part, it, g_lo, g_hi, tag):
+        def out1_matmul(part, i_tile, g_lo, g_hi, tag):
             if g_lo == 0:
-                acc1[(part, it)] = psum.tile([P, D], F32, name="acc1", tag=tag)
-            acc = acc1[(part, it)]
+                out1_bank[(part, i_tile)] = psum.tile([P, D], F32, name="out1_acc", tag=tag)
             for g in range(g_lo, g_hi):
-                c = part * NG + g
+                c = part * GROUPS + g
                 nc.tensor.matmul_mx(
-                    out=acc[:],
-                    lhsT=xk[c][0][:, it * P : (it + 1) * P].bitcast(E4),
-                    lhsT_scale=xk[c][1][:, it * P : (it + 1) * P],
-                    rhs=dyk[c][0][:].bitcast(E5),
-                    rhs_scale=dyk[c][1][:],
+                    out=out1_bank[(part, i_tile)][:],
+                    lhsT=xn_mx[c][0][:, i_tile * P : (i_tile + 1) * P].bitcast(E4M3),
+                    lhsT_scale=xn_mx[c][1][:, i_tile * P : (i_tile + 1) * P],
+                    rhs=dy_mx[c][0][:].bitcast(E5M2),
+                    rhs_scale=dy_mx[c][1][:],
                     start=(g == 0),
-                    stop=(g == NG - 1),
+                    stop=(g == GROUPS - 1),
                 )
 
-        def e1(part, it):
-            o1 = work.tile([P, D], F32, name="o1", tag="o1", bufs=4)
-            nc.scalar.copy(out=o1[:], in_=acc1.pop((part, it))[:])
-            nc.scalar.dma_start(out=out_1[part, it * P : (it + 1) * P, :], in_=o1[:])
+        def out1_finish(part, i_tile):
+            result = work.tile([P, D], F32, name="out1_rows", tag="out1_rows", bufs=4)
+            nc.scalar.copy(out=result[:], in_=out1_bank.pop((part, i_tile))[:])
+            nc.scalar.dma_start(out=out_1[part, i_tile * P : (i_tile + 1) * P, :], in_=result[:])
 
-        il_mid = IL_V_COLS + (D - IL_V_COLS) // 2
-        for s in range(-L_YT, NB + S_E0 + 1):
-            c, r = divmod(s + L_YT - PACK, PACK)
-            if r == 0 and c >= 1 and c + Y_BUFS < NCH:
+        xn_slot = [XN_FIRST + (n * XN_SLOTS) // XN_PIECES for n in range(2 * CHUNKS)]
+
+        def chunk_at(slot, offset):
+            c, r = divmod(slot - offset, PACK)
+            return c if (r == 0 and 0 <= c < CHUNKS) else None
+
+        for slot in range(-LEAD_Y_TRANSPOSE, BLOCKS - PACK + AT_OUT0_FINISH + PACK):
+            c = chunk_at(slot, PACK - LEAD_Y_TRANSPOSE)
+            if c is not None and c >= 1 and c + Y_BUFS < CHUNKS:
                 load_y(c + Y_BUFS)
-            c, r = divmod(s - S_E0 - PACK, PACK)
-            if r == 0 and c >= 0 and c + G_BUFS < NCH:
+            c = chunk_at(slot, AT_OUT0_FINISH + PACK)
+            if c is not None and c + G_BUFS < CHUNKS:
                 load_g(c + G_BUFS)
-            c, r = divmod(s - S_XN - 2, PACK)
-            if r == 0 and c >= 0 and c + X_BUFS < NCH:
-                load_x(c + X_BUFS)
-            if 0 <= s - L_MT < NB:
-                pe_mt(s - L_MT)
-            if 0 <= s + L_YT < NB:
-                pe_yt(s + L_YT)
-            if s in S_W:
-                w_pe(S_W.index(s))
-            c, r = divmod(s - S_E, PACK)
-            if r == 0 and 0 <= c < NCH:
-                pe_e(c)
-            c, j = divmod(s - S_MX, PACK)
-            if 0 <= c < NCH:
-                pe_mx0(c, j)
-            if s in O0_SLOTS:
-                pe_o(0, O0_SLOTS.index(s), 0, NG, "wT")
-            if O1_START <= s < O1_START + PACK:
-                pe_o(1, s - O1_START, 0, NG - 1, "yT" if s - O1_START < 2 else "mT")
-            if s == O1_FIN:
-                for it in range(PACK):
-                    pe_o(1, it, NG - 1, NG, "")
-            if 0 <= s + L_ACT < NB:
-                s_act(s + L_ACT)
-            c, h = divmod(s - S_XN, PACK)
-            if h < 2 and 0 <= c < NCH:
-                xn(c, h)
-            c, jp = divmod(s - S_E, PACK)
-            if jp < 2 and 0 <= c < NCH:
-                ev(c, jp, "s")
-                if jp == 0:
-                    il(c, IL_V_COLS, il_mid, "s")
-                else:
-                    il(c, il_mid, D, "s")
-            if s - 1 in S_W:
-                w_ev(S_W.index(s - 1), 1, "s")
-            if s in O0_SLOTS:
-                e1(0, O0_SLOTS.index(s))
-            if s == O1_FIN:
-                for it in range(PACK):
-                    e1(1, it)
-            if 0 <= s < NB:
-                v_bp(s)
-            c, j = divmod(s - S_E0, PACK)
-            if 0 <= c < NCH:
-                v_e0(c, j)
-            if 0 <= s - L_DY < NB:
-                v_dy(s - L_DY)
-            if 0 <= s < NB:
-                v_m(s)
-            if s in S_W:
-                w_ev(S_W.index(s), 0, "v")
-            if s - 2 in S_W:
-                w_quant(S_W.index(s - 2))
-            c, r = divmod(s - S_E, PACK)
-            if r == 0 and 0 <= c < NCH:
-                il(c, 0, IL_V_COLS, "v")
-            c, r = divmod(s - S_QT, PACK)
-            if r == 0 and 0 <= c < NCH:
-                v_q_dyT(c)
-            c, r = divmod(s - S_QK, PACK)
-            if r == 0 and 0 <= c < NCH:
-                v_q_dq(c)
-            c, r = divmod(s - S_QX, PACK)
-            if r == 0 and 0 <= c < NCH:
-                v_q_x(c)
+            for c in range(CHUNKS - X_BUFS):
+                if slot == xn_slot[2 * c + 1] + 1:
+                    load_x(c + X_BUFS)
+
+            if 0 <= slot - LAG_M_TRANSPOSE < BLOCKS:
+                transpose_m(slot - LAG_M_TRANSPOSE)
+            if 0 <= slot + LEAD_Y_TRANSPOSE < BLOCKS:
+                transpose_y(slot + LEAD_Y_TRANSPOSE)
+            if slot in AT_WEIGHTS:
+                transpose_weights(AT_WEIGHTS.index(slot))
+            c = chunk_at(slot, AT_DY_TRANSPOSE)
+            if c is not None:
+                transpose_dy(c)
+            c, j = divmod(slot - AT_OUT0_MATMUL, PACK)
+            if 0 <= c < CHUNKS:
+                out0_matmul(c, j)
+            if slot in AT_OUT1_PART0:
+                out1_matmul(0, AT_OUT1_PART0.index(slot), 0, GROUPS, "dT")
+            if 0 <= slot - AT_OUT1_PART1 < PACK:
+                i_tile = slot - AT_OUT1_PART1
+                out1_matmul(1, i_tile, 0, GROUPS - 1, "yT" if i_tile < 2 else "mT")
+            if slot == AT_OUT1_LAST:
+                for i_tile in range(PACK):
+                    out1_matmul(1, i_tile, GROUPS - 1, GROUPS, "")
+
+            if 0 <= slot + LEAD_ACTIVATION < BLOCKS:
+                activations(slot + LEAD_ACTIVATION)
+            for n in range(2 * CHUNKS):
+                if slot == xn_slot[n]:
+                    make_x_norm(n // 2, n % 2)
+            c, v = divmod(slot - AT_DY_COPY, PACK)
+            if v < 2 and 0 <= c < CHUNKS:
+                copy_dyT(c, v)
+            if slot - 1 in AT_WEIGHTS:
+                copy_weights(AT_WEIGHTS.index(slot - 1), 1, "scalar")
+            if slot in AT_OUT1_PART0:
+                out1_finish(0, AT_OUT1_PART0.index(slot))
+            if slot == AT_OUT1_LAST:
+                for i_tile in range(PACK):
+                    out1_finish(1, i_tile)
+
+            if 0 <= slot + LEAD_FACTOR < BLOCKS:
+                factor(slot + LEAD_FACTOR)
+            c, j = divmod(slot - AT_OUT0_FINISH, PACK)
+            if 0 <= c < CHUNKS:
+                out0_finish(c, j)
+            if 0 <= slot - LAG_DY < BLOCKS:
+                make_dy(slot - LAG_DY)
+            if 0 <= slot < BLOCKS:
+                make_m(slot)
+            if slot in AT_WEIGHTS:
+                copy_weights(AT_WEIGHTS.index(slot), 0, "vector")
+            if slot - 2 in AT_WEIGHTS:
+                quantize_weights(AT_WEIGHTS.index(slot - 2))
+            c = chunk_at(slot, AT_QUANT_FEATURES)
+            if c is not None:
+                quantize_dy_features(c)
+            c = chunk_at(slot, AT_QUANT_TOKENS)
+            if c is not None:
+                quantize_dy_tokens(c)
+            for c in range(CHUNKS):
+                if slot == xn_slot[2 * c + 1] + XN_QUANT_LAG:
+                    quantize_x_norm(c)

from contextlib import ExitStack

import concourse.mybir as mybir
from concourse.masks import make_identity

FLOPS = 2 * 2 * 2 * 2048 * 512 * 512

F32 = mybir.dt.float32
BF16 = mybir.dt.bfloat16
U32 = mybir.dt.uint32
U8 = mybir.dt.uint8
E4M3 = mybir.dt.float8_e4m3fn_x4
E5M2 = mybir.dt.float8_e5m2_x4
ACT = mybir.ActivationFunctionType
ALU = mybir.AluOpType

P = 128
PACK = 4
D = 512
PARTS = 2
GROUPS = 4
CHUNKS = PARTS * GROUPS
BLOCKS = CHUNKS * PACK

Y_BUFS = 4
G_BUFS = 5
X_BUFS = 3

LEAD_Y_TRANSPOSE = 3
LEAD_ACTIVATION = 2
LEAD_FACTOR = 1
LAG_M_TRANSPOSE = 1
LAG_DY = 2
AT_QUANT_TOKENS = 6
AT_DY_TRANSPOSE = 6
AT_DY_COPY = 7
AT_QUANT_FEATURES = 9
AT_OUT0_MATMUL = 10
AT_OUT0_FINISH = 11
XN_FIRST = 9
XN_PIECES = 5
XN_SLOTS = 8
XN_QUANT_LAG = 2
AT_WEIGHTS = (4, 6)
AT_OUT1_PART0 = (24, 25, 28, 29)
AT_OUT1_PART1 = 34
AT_OUT1_LAST = 38


def tile_better_transformer_t_v_kernel(
    tc, x, weights, bias, gain, norm_bias, gamma, beta, y, grad_out, out_0, out_1
):
    nc = tc.nc

    y_view = y.rearrange("(g p j) w -> p g j w", p=P, j=PACK)
    g_view = grad_out.rearrange("(g p j) w -> p g j w", p=P, j=PACK)
    x_view = x.rearrange("(g p j) w -> p g j w", p=P, j=PACK)
    out0_view = out_0.rearrange("(g p j) w -> p g j w", p=P, j=PACK)
    w_view = weights.rearrange("a (t p) o -> p a t o", p=P)

    with ExitStack() as ctx:
        const = ctx.enter_context(tc.tile_pool(name="const", bufs=1))
        keep = ctx.enter_context(tc.tile_pool(name="keep", bufs=1))
        raw = ctx.enter_context(tc.tile_pool(name="raw", bufs=2))
        work = ctx.enter_context(tc.tile_pool(name="work", bufs=2))
        psum = ctx.enter_context(tc.psum_pool(name="psum", bufs=2))

        y_raw = {}
        g_raw = {}
        x_raw = {}
        w_raw = {}

        def part_columns(part):
            return slice(part * D, (part + 1) * D)

        def load_y(c):
            part, g = divmod(c, GROUPS)
            if c == 0:
                y_raw[0] = []
                for b in range(PACK):
                    t = raw.tile([P, PACK, P], F32, name="y_first", tag="y_first", bufs=PACK)
                    nc.sync.dma_start(out=t[:], in_=y_view[:, 0, :, b * P : (b + 1) * P])
                    y_raw[0].append(t)
            else:
                t = raw.tile([P, PACK, D], F32, name="y_raw", tag="y", bufs=Y_BUFS)
                nc.sync.dma_start(out=t[:], in_=y_view[:, g, :, part_columns(part)])
                y_raw[c] = t

        def y_block(c, b, j):
            if c == 0:
                return y_raw[0][b][:, j, :]
            return y_raw[c][:, j, b * P : (b + 1) * P]

        def load_g(c):
            part, g = divmod(c, GROUPS)
            t = raw.tile([P, PACK, D], BF16, name="g_raw", tag="g", bufs=G_BUFS)
            nc.sync.dma_start(out=t[:], in_=g_view[:, g, :, part_columns(part)])
            g_raw[c] = t

        def load_x(c):
            part, g = divmod(c, GROUPS)
            t = raw.tile([P, PACK, D], BF16, name="x_raw", tag="x", bufs=X_BUFS)
            nc.sync.dma_start(out=t[:], in_=x_view[:, g, :, part_columns(part)])
            x_raw[c] = t

        def load_w(part):
            t = const.tile([P, PACK, D], BF16, name="w_raw%d" % part)
            nc.sync.dma_start(out=t[:], in_=w_view[:, part, :, :])
            w_raw[part] = t

        zero = const.tile([P, 1], F32, name="zero")
        nc.vector.memset(zero[:], 0.0)
        vectors = const.tile([P, P], BF16, name="vectors")
        nc.vector.memset(vectors[:], 0.0)
        nc.sync.dma_start(out=vectors[0:8, :], in_=beta.rearrange("(i f) -> i f", f=P))
        nc.sync.dma_start(out=vectors[8:16, :], in_=gamma.rearrange("(i f) -> i f", f=P))
        gain_bf = const.tile([P, 1], BF16, name="gain_bf")
        nc.sync.dma_start(out=gain_bf[:], in_=gain.partition_broadcast(P))
        nbias_bf = const.tile([P, 1], BF16, name="nbias_bf")
        nc.sync.dma_start(out=nbias_bf[:], in_=norm_bias.partition_broadcast(P))
        table_warm = const.tile([P, 1], F32, name="table_warm")
        nc.scalar.activation(out=table_warm[:], in_=zero[:], func=ACT.Silu)

        load_y(0)
        load_g(0)
        load_y(1)
        load_w(0)
        load_g(1)
        load_y(2)
        load_w(1)
        load_x(0)
        load_g(2)
        load_x(1)
        load_y(3)
        load_g(3)
        load_x(2)
        load_y(4)
        load_g(4)

        ident_f32 = const.tile([P, P], F32, name="ident_f32")
        make_identity(nc, ident_f32[:])
        ident_bf = const.tile([P, P], BF16, name="ident_bf")
        make_identity(nc, ident_bf[:])

        vectors_T = psum.tile([P, P], BF16, name="vectors_T", tag="dT")
        nc.tensor.transpose(vectors_T[:], vectors[:], ident_bf[:])
        beta_col = const.tile([P, 8], F32, name="beta_col")
        nc.vector.tensor_copy(out=beta_col[:], in_=vectors_T[:, 0:8])
        half_beta_col = const.tile([P, 8], F32, name="half_beta_col")
        nc.vector.tensor_scalar(
            out=half_beta_col[:], in0=vectors_T[:, 0:8], scalar1=0.5, scalar2=None, op0=ALU.mult
        )
        factor_col = const.tile([P, 8], F32, name="factor_col")
        nc.vector.tensor_scalar(
            out=factor_col[:], in0=vectors_T[:, 8:16], scalar1=-1.0, scalar2=0.5, op0=ALU.add, op1=ALU.mult
        )
        gain_col = const.tile([P, 1], F32, name="gain_col")
        nc.vector.tensor_copy(out=gain_col[:], in_=gain_bf[:])
        nbias_col = const.tile([P, 1], F32, name="nbias_col")
        nc.vector.tensor_copy(out=nbias_col[:], in_=nbias_bf[:])

        w_bank = {}
        w_grouped = {}
        w_mx = {}

        def transpose_weights(part):
            w_grouped[part] = work.tile([P, D, PACK], BF16, name="w_grouped", tag="w_grouped", bufs=2, align_bytes=64)
            for h in range(2):
                bank = psum.tile([P, 2, 2 * P], F32, name="w_T", tag="dT" if part == 0 else "acc")
                for u in range(2):
                    for t in range(2):
                        words = w_raw[part][:, 2 * h + t, :].bitcast(F32)
                        nc.tensor.transpose(bank[:, u, t * P : (t + 1) * P], words[:, u : D // 2 : 2], ident_f32[:])
                w_bank[(part, h)] = bank

        def copy_weights(part, h, engine):
            dst = w_grouped[part][:, h * 2 * P : (h + 1) * 2 * P, :]
            dst = dst.rearrange("q i t -> q (i t)").bitcast(F32).rearrange("q (i u) -> q i u", u=2)
            src = w_bank.pop((part, h))[:].rearrange("q u i -> q i u")
            if engine == "scalar":
                nc.scalar.copy(out=dst, in_=src)
            else:
                nc.vector.tensor_copy(out=dst, in_=src)

        def quantize_weights(part):
            codes = keep.tile([P, D], U32, name="w_codes%d" % part, align_bytes=64)
            scales = keep.tile([P, D], U8, name="w_scales%d" % part, align_bytes=64)
            nc.vector.quantize_mx(
                out=codes[:].bitcast(E4M3), scales=scales[:], in_=w_grouped[part][:].rearrange("q i t -> q (i t)")
            )
            w_mx[part] = (codes, scales)

        y_bank = {}
        tanh_tile = {}
        silu_tile = {}
        m_bank = {}
        dy_tile = {}

        def vector_column(k):
            return (k // (PACK * GROUPS)) * PACK + k % PACK

        def transpose_y(k):
            c, b = divmod(k, PACK)
            bank = psum.tile([P, PACK, P], F32, name="y_T", tag="yT")
            for j in range(PACK):
                nc.tensor.transpose(bank[:, j, :], y_block(c, b, j), ident_f32[:])
            y_bank[k] = bank

        def activations(k):
            i = vector_column(k)
            yT = y_bank.pop(k)[:].rearrange("f j p -> f (j p)")
            s = work.tile([P, D], F32, name="silu", tag="silu", bufs=5)
            nc.scalar.activation(out=s[:], in_=yT, func=ACT.Silu, scale=beta_col[:, i : i + 1])
            t = work.tile([P, D], F32, name="tanh", tag="tanh", bufs=6)
            nc.scalar.activation(out=t[:], in_=yT, func=ACT.Tanh, scale=half_beta_col[:, i : i + 1])
            silu_tile[k] = s
            tanh_tile[k] = t

        def factor(k):
            i = vector_column(k)
            s = silu_tile[k]
            nc.vector.tensor_scalar(
                out=s[:], in0=s[:], scalar1=-1.0, scalar2=factor_col[:, i : i + 1], op0=ALU.add, op1=ALU.mult
            )

        def make_m(k):
            t = tanh_tile[k]
            nc.vector.scalar_tensor_tensor(
                out=t[:], in0=t[:], scalar=-1.0, in1=silu_tile.pop(k)[:], op0=ALU.add, op1=ALU.mult
            )

        def transpose_m(k):
            bank = psum.tile([P, PACK, P], F32, name="m_T", tag="mT")
            m = tanh_tile.pop(k)
            for j in range(PACK):
                nc.tensor.transpose(bank[:, j, :], m[:, j * P : (j + 1) * P], ident_f32[:])
            m_bank[k] = bank

        def make_dy(k):
            c, b = divmod(k, PACK)
            if b == 0:
                dy_tile[c] = work.tile([P, D, PACK], BF16, name="dy", tag="dy", bufs=3, align_bytes=64)
            nc.vector.scalar_tensor_tensor(
                out=dy_tile[c][:, b * P : (b + 1) * P, :],
                in0=m_bank.pop(k)[:].rearrange("p j f -> p f j"),
                scalar=1.0,
                in1=g_raw[c][:, :, b * P : (b + 1) * P].rearrange("p j f -> p f j"),
                op0=ALU.add,
                op1=ALU.mult,
            )

        dyT_bank = {}
        dyT_grouped = {}
        dyT_mx = {}
        dy_mx = {}
        xn_tile = {}
        xn_mx = {}
        out0_bank = {}
        out1_bank = {}

        def transpose_dy(c):
            words = dy_tile[c][:].rearrange("p f j -> p (f j)").bitcast(F32)
            dyT_grouped[c] = work.tile([P, D, PACK], BF16, name="dyT_grouped", tag="dyT_grouped", bufs=2, align_bytes=64)
            for v in range(2):
                bank = psum.tile([P, PACK, P], F32, name="dy_T", tag="dT")
                for t in range(PACK):
                    nc.tensor.transpose(bank[:, t, :], words[:, 2 * t + v : 2 * D : 2 * PACK], ident_f32[:])
                dyT_bank[(c, v)] = bank

        def copy_dyT(c, v):
            dst = dyT_grouped[c][:, v * 2 * P : (v + 1) * 2 * P, :].rearrange("q (e p) t -> q e p t", e=2)
            src = dyT_bank.pop((c, v))[:].rearrange("q t p -> q (t p)").bitcast(BF16)
            nc.scalar.copy(out=dst, in_=src.rearrange("q (t p e) -> q e p t", t=PACK, e=2))

        def quantize_dy_features(c):
            codes = work.tile([P, D], U32, name="dyT_codes", tag="dyT_codes", bufs=2, align_bytes=64)
            scales = work.tile([P, D], U8, name="dyT_scales", tag="dyT_scales", bufs=2, align_bytes=64)
            nc.vector.quantize_mx(
                out=codes[:].bitcast(E5M2),
                scales=scales[:],
                in_=dyT_grouped.pop(c)[:].rearrange("q r t -> q (r t)"),
            )
            dyT_mx[c] = (codes, scales)

        def quantize_dy_tokens(c):
            codes = keep.tile([P, D], U32, name="dy_codes%d" % c, align_bytes=64)
            scales = keep.tile([P, D], U8, name="dy_scales%d" % c, align_bytes=64)
            nc.vector.quantize_mx(
                out=codes[:].bitcast(E5M2), scales=scales[:], in_=dy_tile[c][:].rearrange("p f j -> p (f j)")
            )
            dy_mx[c] = (codes, scales)

        def out0_matmul(c, j):
            part = c // GROUPS
            codes, scales = dyT_mx[c]
            bank = psum.tile([P, D], F32, name="out0_acc", tag="dT" if (c == CHUNKS - 1 and j >= 2) else "acc")
            nc.tensor.matmul_mx(
                out=bank[:],
                lhsT=codes[:, j * P : (j + 1) * P].bitcast(E5M2),
                lhsT_scale=scales[:, j * P : (j + 1) * P],
                rhs=w_mx[part][0][:].bitcast(E4M3),
                rhs_scale=w_mx[part][1][:],
                start=True,
                stop=True,
            )
            out0_bank[(c, j)] = bank

        def out0_finish(c, j):
            part, g = divmod(c, GROUPS)
            result = work.tile([P, D], F32, name="out0_rows", tag="out0_rows", bufs=6)
            nc.vector.scalar_tensor_tensor(
                out=result[:],
                in0=out0_bank.pop((c, j))[:],
                scalar=gain_col[:, 0:1],
                in1=g_raw[c][:, j, :],
                op0=ALU.mult,
                op1=ALU.add,
            )
            nc.sync.dma_start(out=out0_view[:, g, j, part_columns(part)], in_=result[:])

        def make_x_norm(c, half):
            if half == 0:
                xn_tile[c] = work.tile([P, D, PACK], BF16, name="x_norm", tag="x_norm", bufs=2, align_bytes=64)
            lo = half * (D // 2)
            hi = lo + D // 2
            nc.scalar.activation(
                out=xn_tile[c][:, lo:hi, :],
                in_=x_raw[c][:, :, lo:hi].rearrange("p j f -> p f j"),
                func=ACT.Identity,
                scale=gain_col[:, 0:1],
                bias=nbias_col[:, 0:1],
            )

        def quantize_x_norm(c):
            codes = keep.tile([P, D], U32, name="xn_codes%d" % c, align_bytes=64)
            scales = keep.tile([P, D], U8, name="xn_scales%d" % c, align_bytes=64)
            nc.vector.quantize_mx(
                out=codes[:].bitcast(E4M3), scales=scales[:], in_=xn_tile.pop(c)[:].rearrange("p f j -> p (f j)")
            )
            xn_mx[c] = (codes, scales)

        def out1_matmul(part, i_tile, g_lo, g_hi, tag):
            if g_lo == 0:
                out1_bank[(part, i_tile)] = psum.tile([P, D], F32, name="out1_acc", tag=tag)
            for g in range(g_lo, g_hi):
                c = part * GROUPS + g
                nc.tensor.matmul_mx(
                    out=out1_bank[(part, i_tile)][:],
                    lhsT=xn_mx[c][0][:, i_tile * P : (i_tile + 1) * P].bitcast(E4M3),
                    lhsT_scale=xn_mx[c][1][:, i_tile * P : (i_tile + 1) * P],
                    rhs=dy_mx[c][0][:].bitcast(E5M2),
                    rhs_scale=dy_mx[c][1][:],
                    start=(g == 0),
                    stop=(g == GROUPS - 1),
                )

        def out1_finish(part, i_tile):
            result = work.tile([P, D], F32, name="out1_rows", tag="out1_rows", bufs=4)
            nc.scalar.copy(out=result[:], in_=out1_bank.pop((part, i_tile))[:])
            nc.scalar.dma_start(out=out_1[part, i_tile * P : (i_tile + 1) * P, :], in_=result[:])

        xn_slot = [XN_FIRST + (n * XN_SLOTS) // XN_PIECES for n in range(2 * CHUNKS)]

        def chunk_at(slot, offset):
            c, r = divmod(slot - offset, PACK)
            return c if (r == 0 and 0 <= c < CHUNKS) else None

        for slot in range(-LEAD_Y_TRANSPOSE, BLOCKS - PACK + AT_OUT0_FINISH + PACK):
            c = chunk_at(slot, PACK - LEAD_Y_TRANSPOSE)
            if c is not None and c >= 1 and c + Y_BUFS < CHUNKS:
                load_y(c + Y_BUFS)
            c = chunk_at(slot, AT_OUT0_FINISH + PACK)
            if c is not None and c + G_BUFS < CHUNKS:
                load_g(c + G_BUFS)
            for c in range(CHUNKS - X_BUFS):
                if slot == xn_slot[2 * c + 1] + 1:
                    load_x(c + X_BUFS)

            if 0 <= slot - LAG_M_TRANSPOSE < BLOCKS:
                transpose_m(slot - LAG_M_TRANSPOSE)
            if 0 <= slot + LEAD_Y_TRANSPOSE < BLOCKS:
                transpose_y(slot + LEAD_Y_TRANSPOSE)
            if slot in AT_WEIGHTS:
                transpose_weights(AT_WEIGHTS.index(slot))
            c = chunk_at(slot, AT_DY_TRANSPOSE)
            if c is not None:
                transpose_dy(c)
            c, j = divmod(slot - AT_OUT0_MATMUL, PACK)
            if 0 <= c < CHUNKS:
                out0_matmul(c, j)
            if slot in AT_OUT1_PART0:
                out1_matmul(0, AT_OUT1_PART0.index(slot), 0, GROUPS, "dT")
            if 0 <= slot - AT_OUT1_PART1 < PACK:
                i_tile = slot - AT_OUT1_PART1
                out1_matmul(1, i_tile, 0, GROUPS - 1, "yT" if i_tile < 2 else "mT")
            if slot == AT_OUT1_LAST:
                for i_tile in range(PACK):
                    out1_matmul(1, i_tile, GROUPS - 1, GROUPS, "")

            if 0 <= slot + LEAD_ACTIVATION < BLOCKS:
                activations(slot + LEAD_ACTIVATION)
            for n in range(2 * CHUNKS):
                if slot == xn_slot[n]:
                    make_x_norm(n // 2, n % 2)
            c, v = divmod(slot - AT_DY_COPY, PACK)
            if v < 2 and 0 <= c < CHUNKS:
                copy_dyT(c, v)
            if slot - 1 in AT_WEIGHTS:
                copy_weights(AT_WEIGHTS.index(slot - 1), 1, "scalar")
            if slot in AT_OUT1_PART0:
                out1_finish(0, AT_OUT1_PART0.index(slot))
            if slot == AT_OUT1_LAST:
                for i_tile in range(PACK):
                    out1_finish(1, i_tile)

            if 0 <= slot + LEAD_FACTOR < BLOCKS:
                factor(slot + LEAD_FACTOR)
            c, j = divmod(slot - AT_OUT0_FINISH, PACK)
            if 0 <= c < CHUNKS:
                out0_finish(c, j)
            if 0 <= slot - LAG_DY < BLOCKS:
                make_dy(slot - LAG_DY)
            if 0 <= slot < BLOCKS:
                make_m(slot)
            if slot in AT_WEIGHTS:
                copy_weights(AT_WEIGHTS.index(slot), 0, "vector")
            if slot - 2 in AT_WEIGHTS:
                quantize_weights(AT_WEIGHTS.index(slot - 2))
            c = chunk_at(slot, AT_QUANT_FEATURES)
            if c is not None:
                quantize_dy_features(c)
            c = chunk_at(slot, AT_QUANT_TOKENS)
            if c is not None:
                quantize_dy_tokens(c)
            for c in range(CHUNKS):
                if slot == xn_slot[2 * c + 1] + XN_QUANT_LAG:
                    quantize_x_norm(c)
